import numpy as np
import ml_dtypes


def mxq(x, axis, fmt="e4m3"):
    dtype, down = {"e4m3": (ml_dtypes.float8_e4m3fn, 7), "e5m2": (ml_dtypes.float8_e5m2, 14)}[fmt]
    v = np.moveaxis(np.asarray(x, np.float32).astype(ml_dtypes.bfloat16).astype(np.float64), axis, -1)
    blocks = v.reshape(v.shape[:-1] + (-1, 32))
    amax = np.abs(blocks).max(-1, keepdims=True)
    byte = np.maximum(np.where(amax > 0, np.frexp(amax)[1] - 1 + 127, 0) - down, 1)
    scale = np.exp2(byte - 127.0)
    codes = (blocks / scale).astype(np.float32).astype(dtype).astype(np.float64)
    return np.moveaxis((codes * scale).reshape(v.shape), -1, axis)


WIDE = False


def mx_kscale(k):
    if not WIDE:
        return np.ones(k)
    levels = np.array([10, -10, 5, -5, 0])
    a = np.random.permutation(np.resize(levels, k // 512 * 4)).reshape(k // 512, 4)
    idx = np.arange(k)
    return np.exp2(a[idx // 512, idx % 128 // 32])


BF16 = ml_dtypes.bfloat16


def bf(x):
    return np.asarray(x, np.float32).astype(BF16)


def f64(x):
    return np.asarray(x).astype(np.float64)


E2M1 = np.array([0.0, 0.5, 1.0, 1.5, 2.0, 3.0, 4.0, 6.0, -0.0, -0.5, -1.0, -1.5, -2.0, -3.0, -4.0, -6.0])


def pack_weight(w, fmt):
    k, n = w.shape
    w = f64(bf(w)).reshape(k // 32, 32, n)
    amax = np.abs(w).max(1)
    if fmt == "e4m3":
        byte = np.frexp(amax)[1] - 1 + 127 - 7
    else:
        mant, ex = np.frexp(amax / 6.0)
        byte = np.where(mant > 0.5, ex, ex - 1) + 127
    byte = np.clip(np.where(amax > 0, byte, 1), 1, 254)
    scaled = (w * np.exp2(127.0 - byte)[:, None, :]).reshape(k, n).astype(np.float32)
    by_word = np.ascontiguousarray(scaled.reshape(k // 512, 128, 4, n).transpose(0, 1, 3, 2))
    if fmt == "e4m3":
        words = by_word.astype(ml_dtypes.float8_e4m3fn).view(np.uint8)
    else:
        c = by_word.astype(ml_dtypes.float4_e2m1fn).view(np.uint8) & 0xF
        words = c[..., 0::2] | (c[..., 1::2] << 4)
    return np.ascontiguousarray(words), np.ascontiguousarray(byte.astype(np.uint8).reshape(k // 512, 16, n))


def unpack_weight(words, scales, fmt):
    g, p, n, _ = words.shape
    if fmt == "e4m3":
        vals = np.ascontiguousarray(words).view(ml_dtypes.float8_e4m3fn).astype(np.float64)
    else:
        nib = np.empty((g, p, n, 4), np.uint8)
        nib[..., 0::2] = words & 0xF
        nib[..., 1::2] = words >> 4
        vals = E2M1[nib]
    vals = vals * np.repeat(np.exp2(scales.astype(np.float64) - 127.0), 8, axis=1)[..., None]
    return vals.transpose(0, 1, 3, 2).reshape(g * 512, n)


B, L, C, K = 512, 8, 512, 5
F = C
BN_EPS = 1e-3
LEAKY_ALPHA = 0.3


def leaky(v):
    return np.where(v >= 0, v, LEAKY_ALPHA * v)


def bn(v, gamma, beta, mean, var):
    return gamma * (v - mean) * (1.0 / np.sqrt(var + BN_EPS)) + beta


def setup_inputs():
    s = mx_kscale(C)
    x = bf(np.random.standard_normal((B, L, C)) * s)
    k1 = np.random.standard_normal((K, L, C, F)) * 0.14 / np.sqrt(K * C) / s[:, None]
    k1_words, k1_scales = pack_weight(k1.reshape(-1, F), "e4m3")
    return {"x": x,
            "k1_words": k1_words,
            "k1_scales": k1_scales,
            "b1": bf(np.random.standard_normal((L, F)) * 0.03),
            "gamma1": bf(1.0 + 0.1 * np.random.standard_normal(F)),
            "beta1": bf(np.random.standard_normal(F) * 0.2),
            "mean1": bf(np.random.standard_normal(F) * 0.05),
            "var1": bf(np.random.uniform(0.01, 0.03, F))}


def reference(x, k1_words, k1_scales, b1, gamma1, beta1, mean1, var1):
    xq = mxq(f64(x).transpose(1, 0, 2), 2, "e4m3")
    k = unpack_weight(k1_words, k1_scales, "e4m3").reshape(K, L, C, F)
    out = 2.0 * f64(b1)
    for i in range(k.shape[0]):
        step = (i // 2) * (-1 if i % 2 == 1 else 1)
        ki = k[i][(np.arange(L) + step) % L] if step != 0 else k[i]
        p = xq @ ki
        p = np.roll(p, step, axis=0) if step != 0 else p
        out = out + p.transpose(1, 0, 2)
    return leaky(bn(out, f64(gamma1), f64(beta1), f64(mean1), f64(var1)))

@@ -1,0 +1,178 @@
+from contextlib import ExitStack
+
+import concourse.mybir as mybir
+from concourse.masks import make_identity
+
+F32 = mybir.dt.float32
+BF16 = mybir.dt.bfloat16
+I32 = mybir.dt.int32
+U32 = mybir.dt.uint32
+U8 = mybir.dt.uint8
+FP8X4 = mybir.dt.float8_e4m3fn_x4
+ALU = mybir.AluOpType
+
+P = 128
+PACK = 4
+B, L, C, F = 512, 8, 512, 512
+TAP_STEP = (0, 0, 1, -1, 2)
+TAPS = len(TAP_STEP)
+B_TILES = B // P
+F_TILES = F // P
+HALF = L // 2
+BN_EPS = 1e-3
+LEAKY_ALPHA = 0.3
+
+FLOPS = 2 * TAPS * L * B * C * F
+
+ROW_GAMMA, ROW_BETA, ROW_MEAN, ROW_VAR, ROWS = 8, 9, 10, 11, 16
+GAIN = L
+
+
+def tile_residualblock5_pa_t_e_kernel(tc, x, k1_words, k1_scales, b1, gamma1, beta1, mean1, var1, out):
+    nc = tc.nc
+    positions = [2] + [l for l in range(L) if l != 2]
+
+    with ExitStack() as ctx:
+        keep = ctx.enter_context(tc.tile_pool(name="keep", bufs=1))
+        stage = ctx.enter_context(tc.tile_pool(name="stage", bufs=3))
+        results = ctx.enter_context(tc.tile_pool(name="results", bufs=6))
+        psum_tr = ctx.enter_context(tc.psum_pool(name="psum_tr", bufs=3))
+        psum_acc = ctx.enter_context(tc.psum_pool(name="psum_acc", bufs=5))
+
+        x_sb = keep.tile([P, B_TILES, L, C], BF16)
+        x_codes = keep.tile([P, B_TILES, L, P], U32, align_bytes=64)
+        x_scales = keep.tile([P, B_TILES, L, P], U8, align_bytes=64)
+        w_codes = keep.tile([P, L, TAPS, F], U32, align_bytes=64)
+        w_scales = keep.tile([P, 2, TAPS, F], U8, align_bytes=64)
+        ident = keep.tile([P, P], F32)
+        raw_bf = keep.tile([P, F], BF16)
+        raw = keep.tile([P, F], F32)
+        cols = keep.tile([P, F_TILES, ROWS], F32)
+        var_eps = keep.tile([P, F_TILES], F32)
+        std = keep.tile([P, F_TILES], F32)
+        rstd = keep.tile([P, F_TILES], F32)
+        spread = keep.tile([P, F_TILES, L + 1], F32)
+        gain_bc = keep.tile([P, F], F32)
+        shift_bc = keep.tile([P, L, F], F32)
+
+        nc.vector.memset(w_scales[:].rearrange("p h i n -> p (h i n)").bitcast(I32), 0)
+        nc.vector.memset(raw_bf[:], 0.0)
+        make_identity(nc, ident[:])
+
+        nc.scalar.dma_start(out=raw_bf[0:L, :], in_=b1)
+        for row, vec in ((ROW_GAMMA, gamma1), (ROW_BETA, beta1), (ROW_MEAN, mean1), (ROW_VAR, var1)):
+            nc.scalar.dma_start(out=raw_bf[row : row + 1, :], in_=vec.unsqueeze(0))
+
+        x_view = x.rearrange("(m p) l c -> p m l c", p=P)
+        w_view = k1_words.rearrange("(i l) p n t -> l p i (n t)", l=L)
+        s_view = k1_scales.rearrange("(i h j) q n -> h q j i n", h=2, j=HALF)
+        out_view = out.rearrange("(m p) l f -> p m l f", p=P)
+
+        def load_x(half):
+            for m in range(B_TILES):
+                ls = slice(HALF * half, HALF * (half + 1))
+                nc.sync.dma_start(out=x_sb[:, m, ls, :], in_=x_view[:, m, ls, :])
+
+        def load_scales(half):
+            for quad in range(4):
+                for r in range(4):
+                    first = 32 * quad + r
+                    nc.sync.dma_start(
+                        out=w_scales[first : first + 16 : 4, half, :, :].bitcast(I32),
+                        in_=s_view[half, 4 * quad + r].bitcast(I32),
+                    )
+
+        def load_weights(l):
+            nc.sync.dma_start(out=w_codes[:, l, :, :].bitcast(I32), in_=w_view[l].bitcast(I32))
+
+        load_x(0)
+        load_scales(0)
+        load_weights(positions[0])
+        load_x(1)
+        for l in positions[1:HALF]:
+            load_weights(l)
+        load_scales(1)
+        for l in positions[HALF:]:
+            load_weights(l)
+
+        def quantise_x(half):
+            for m in range(B_TILES):
+                grouped = stage.tile([P, HALF, P, PACK], BF16, align_bytes=64)
+                for pair in range(HALF // 2):
+                    xt = psum_tr.tile([P, 2, 2, P], F32, tag="tr")
+                    for li in range(2):
+                        words = x_sb[:, m, HALF * half + 2 * pair + li, :].bitcast(F32)
+                        for u in range(2):
+                            nc.tensor.transpose(xt[:, li, u, :], words[:, u : C // 2 : 2], ident[:])
+                    nc.scalar.copy(
+                        out=grouped[:].bitcast(F32)[:, 2 * pair : 2 * pair + 2, :, :],
+                        in_=xt[:].rearrange("p l u b -> p l b u"),
+                    )
+                ls = slice(HALF * half, HALF * (half + 1))
+                nc.vector.quantize_mx(
+                    out=x_codes[:, m, ls, :].rearrange("p l b -> p (l b)").bitcast(FP8X4),
+                    scales=x_scales[:, m, ls, :].rearrange("p l b -> p (l b)"),
+                    in_=grouped[:].rearrange("p l b t -> p (l b t)"),
+                )
+
+        quantise_x(0)
+
+        nc.vector.tensor_copy(out=raw[:], in_=raw_bf[:])
+        cols_ps = psum_tr.tile([P, F_TILES, P], F32, tag="tr")
+        for j in range(F_TILES):
+            nc.tensor.transpose(cols_ps[:, j, :], raw[:, j * P : (j + 1) * P], ident[:])
+        nc.vector.tensor_copy(out=cols[:], in_=cols_ps[:, :, 0:ROWS])
+        nc.vector.tensor_scalar_add(out=var_eps[:], in0=cols[:, :, ROW_VAR], scalar1=BN_EPS)
+        nc.scalar.sqrt(out=std[:], in_=var_eps[:])
+        nc.vector.reciprocal(out=rstd[:], in_=std[:])
+        nc.vector.tensor_mul(out=spread[:, :, GAIN], in0=cols[:, :, ROW_GAMMA], in1=rstd[:])
+        per_position = [P, F_TILES, L]
+        nc.vector.scalar_tensor_tensor(
+            out=spread[:, :, 0:L],
+            in0=cols[:, :, 0:L],
+            scalar=2.0,
+            in1=cols[:, :, ROW_MEAN : ROW_MEAN + 1].to_broadcast(per_position),
+            op0=ALU.mult,
+            op1=ALU.subtract,
+        )
+        nc.vector.tensor_mul(
+            out=spread[:, :, 0:L], in0=spread[:, :, 0:L], in1=spread[:, :, GAIN : GAIN + 1].to_broadcast(per_position)
+        )
+        nc.vector.tensor_add(
+            out=spread[:, :, 0:L], in0=spread[:, :, 0:L], in1=cols[:, :, ROW_BETA : ROW_BETA + 1].to_broadcast(per_position)
+        )
+        for r in [GAIN] + positions:
+            bc_ps = psum_tr.tile([P, F_TILES, P], F32, tag="tr")
+            for j in range(F_TILES):
+                nc.tensor.transpose(bc_ps[:, j, :], spread[:, j, r : r + 1].to_broadcast([P, P]), ident[:])
+            target = gain_bc[:] if r == GAIN else shift_bc[:, r, :]
+            nc.vector.tensor_copy(out=target, in_=bc_ps[:].rearrange("p j n -> p (j n)"))
+
+        def position(l):
+            z = results.tile([P, B_TILES, F], F32)
+            first_row = PACK * (l % HALF)
+            for m in range(B_TILES):
+                acc = psum_acc.tile([P, F], F32)
+                for i in range(TAPS):
+                    src = (l - TAP_STEP[i]) % L
+                    nc.tensor.matmul_mx(
+                        out=acc[:],
+                        lhsT=x_codes[:, m, src, :].bitcast(FP8X4),
+                        lhsT_scale=x_scales[:, m, src, :],
+                        rhs=w_codes[:, l, i, :].bitcast(FP8X4),
+                        rhs_scale=w_scales[first_row:P, l // HALF, i, :],
+                        start=(i == 0),
+                        stop=(i == TAPS - 1),
+                    )
+                nc.vector.tensor_tensor(out=z[:, m, :], in0=acc[:], in1=gain_bc[:], op=ALU.mult)
+            nc.vector.tensor_tensor(
+                out=z[:], in0=z[:], in1=shift_bc[:, l, :].unsqueeze(1).to_broadcast([P, B_TILES, F]), op=ALU.add
+            )
+            flat = z[:].rearrange("p m f -> p (m f)")
+            nc.vector.scalar_tensor_tensor(out=flat, in0=flat, scalar=LEAKY_ALPHA, in1=flat, op0=ALU.mult, op1=ALU.max)
+            nc.sync.dma_start(out=out_view[:, :, l, :], in_=z[:])
+
+        position(positions[0])
+        quantise_x(1)
+        for l in positions[1:]:
+            position(l)

@@ -10,6 +10,7 @@ U32 = mybir.dt.uint32
 U8 = mybir.dt.uint8
 FP8X4 = mybir.dt.float8_e4m3fn_x4
 ALU = mybir.AluOpType
+ACT = mybir.ActivationFunctionType
 
 P = 128
 PACK = 4
@@ -35,7 +36,8 @@ def tile_residualblock5_pa_t_e_kernel(tc, x, k1_words, k1_scales, b1, gamma1, be
     with ExitStack() as ctx:
         keep = ctx.enter_context(tc.tile_pool(name="keep", bufs=1))
         stage = ctx.enter_context(tc.tile_pool(name="stage", bufs=3))
-        results = ctx.enter_context(tc.tile_pool(name="results", bufs=6))
+        results = ctx.enter_context(tc.tile_pool(name="results", bufs=10))
+        scratch = ctx.enter_context(tc.tile_pool(name="scratch", bufs=3))
         psum_tr = ctx.enter_context(tc.psum_pool(name="psum_tr", bufs=3))
         psum_acc = ctx.enter_context(tc.psum_pool(name="psum_acc", bufs=5))
 
@@ -53,7 +55,6 @@ def tile_residualblock5_pa_t_e_kernel(tc, x, k1_words, k1_scales, b1, gamma1, be
         rstd = keep.tile([P, F_TILES], F32)
         spread = keep.tile([P, F_TILES, L + 1], F32)
         gain_bc = keep.tile([P, F], F32)
-        shift_bc = keep.tile([P, L, F], F32)
 
         nc.vector.memset(w_scales[:].rearrange("p h i n -> p (h i n)").bitcast(I32), 0)
         nc.vector.memset(raw_bf[:], 0.0)
@@ -141,36 +142,42 @@ def tile_residualblock5_pa_t_e_kernel(tc, x, k1_words, k1_scales, b1, gamma1, be
         nc.vector.tensor_add(
             out=spread[:, :, 0:L], in0=spread[:, :, 0:L], in1=cols[:, :, ROW_BETA : ROW_BETA + 1].to_broadcast(per_position)
         )
-        for r in [GAIN] + positions:
-            bc_ps = psum_tr.tile([P, F_TILES, P], F32, tag="tr")
+
+        def spread_row(r):
+            row_ps = psum_tr.tile([P, F_TILES, P], F32, tag="tr")
             for j in range(F_TILES):
-                nc.tensor.transpose(bc_ps[:, j, :], spread[:, j, r : r + 1].to_broadcast([P, P]), ident[:])
-            target = gain_bc[:] if r == GAIN else shift_bc[:, r, :]
-            nc.vector.tensor_copy(out=target, in_=bc_ps[:].rearrange("p j n -> p (j n)"))
+                nc.tensor.transpose(row_ps[:, j, :], spread[:, j, r : r + 1].to_broadcast([P, P]), ident[:])
+            return row_ps[:].rearrange("p j n -> p (j n)")
+
+        nc.vector.tensor_copy(out=gain_bc[:], in_=spread_row(GAIN))
 
         def position(l):
-            z = results.tile([P, B_TILES, F], F32)
+            shift_ps = spread_row(l)
             first_row = PACK * (l % HALF)
-            for m in range(B_TILES):
-                acc = psum_acc.tile([P, F], F32)
-                for i in range(TAPS):
-                    src = (l - TAP_STEP[i]) % L
-                    nc.tensor.matmul_mx(
-                        out=acc[:],
-                        lhsT=x_codes[:, m, src, :].bitcast(FP8X4),
-                        lhsT_scale=x_scales[:, m, src, :],
-                        rhs=w_codes[:, l, i, :].bitcast(FP8X4),
-                        rhs_scale=w_scales[first_row:P, l // HALF, i, :],
-                        start=(i == 0),
-                        stop=(i == TAPS - 1),
-                    )
-                nc.vector.tensor_tensor(out=z[:, m, :], in0=acc[:], in1=gain_bc[:], op=ALU.mult)
-            nc.vector.tensor_tensor(
-                out=z[:], in0=z[:], in1=shift_bc[:, l, :].unsqueeze(1).to_broadcast([P, B_TILES, F]), op=ALU.add
-            )
-            flat = z[:].rearrange("p m f -> p (m f)")
-            nc.vector.scalar_tensor_tensor(out=flat, in0=flat, scalar=LEAKY_ALPHA, in1=flat, op0=ALU.mult, op1=ALU.max)
-            nc.sync.dma_start(out=out_view[:, :, l, :], in_=z[:])
+            for pair in range(B_TILES // 2):
+                z = results.tile([P, 2, F], F32)
+                for k in range(2):
+                    m = 2 * pair + k
+                    acc = psum_acc.tile([P, F], F32)
+                    for i in range(TAPS):
+                        src = (l - TAP_STEP[i]) % L
+                        nc.tensor.matmul_mx(
+                            out=acc[:],
+                            lhsT=x_codes[:, m, src, :].bitcast(FP8X4),
+                            lhsT_scale=x_scales[:, m, src, :],
+                            rhs=w_codes[:, l, i, :].bitcast(FP8X4),
+                            rhs_scale=w_scales[first_row:P, l // HALF, i, :],
+                            start=(i == 0),
+                            stop=(i == TAPS - 1),
+                        )
+                    nc.vector.tensor_tensor(out=z[:, k, :], in0=acc[:], in1=gain_bc[:], op=ALU.mult)
+                nc.vector.tensor_tensor(
+                    out=z[:], in0=z[:], in1=shift_ps.unsqueeze(1).to_broadcast([P, 2, F]), op=ALU.add
+                )
+                lift = scratch.tile([P, 2, F], F32)
+                nc.scalar.activation(out=lift[:], in_=z[:], func=ACT.Relu, scale=LEAKY_ALPHA - 1.0)
+                nc.gpsimd.tensor_tensor(out=z[:], in0=z[:], in1=lift[:], op=ALU.add)
+                nc.sync.dma_start(out=out_view[:, 2 * pair : 2 * pair + 2, l, :], in_=z[:])
 
         position(positions[0])
         quantise_x(1)

@@ -31,12 +31,12 @@ GAIN = L
 
 def tile_residualblock5_pa_t_e_kernel(tc, x, k1_words, k1_scales, b1, gamma1, beta1, mean1, var1, out):
     nc = tc.nc
-    positions = [2] + [l for l in range(L) if l != 2]
 
     with ExitStack() as ctx:
+        ctx.enter_context(tc.manual_schedule())
         keep = ctx.enter_context(tc.tile_pool(name="keep", bufs=1))
         stage = ctx.enter_context(tc.tile_pool(name="stage", bufs=3))
-        results = ctx.enter_context(tc.tile_pool(name="results", bufs=10))
+        results = ctx.enter_context(tc.tile_pool(name="results", bufs=20))
         scratch = ctx.enter_context(tc.tile_pool(name="scratch", bufs=3))
         psum_tr = ctx.enter_context(tc.psum_pool(name="psum_tr", bufs=3))
         psum_acc = ctx.enter_context(tc.psum_pool(name="psum_acc", bufs=5))
@@ -65,14 +65,9 @@ def tile_residualblock5_pa_t_e_kernel(tc, x, k1_words, k1_scales, b1, gamma1, be
             nc.scalar.dma_start(out=raw_bf[row : row + 1, :], in_=vec.unsqueeze(0))
 
         x_view = x.rearrange("(m p) l c -> p m l c", p=P)
-        w_view = k1_words.rearrange("(i l) p n t -> l p i (n t)", l=L)
+        w_view = k1_words.rearrange("(i l) p n t -> l i p (n t)", l=L)
         s_view = k1_scales.rearrange("(i h j) q n -> h q j i n", h=2, j=HALF)
         out_view = out.rearrange("(m p) l f -> p m l f", p=P)
-
-        def load_x(half):
-            for m in range(B_TILES):
-                ls = slice(HALF * half, HALF * (half + 1))
-                nc.sync.dma_start(out=x_sb[:, m, ls, :], in_=x_view[:, m, ls, :])
 
         def load_scales(half):
             for quad in range(4):
@@ -83,40 +78,15 @@ def tile_residualblock5_pa_t_e_kernel(tc, x, k1_words, k1_scales, b1, gamma1, be
                         in_=s_view[half, 4 * quad + r].bitcast(I32),
                     )
 
-        def load_weights(l):
-            nc.sync.dma_start(out=w_codes[:, l, :, :].bitcast(I32), in_=w_view[l].bitcast(I32))
-
-        load_x(0)
-        load_scales(0)
-        load_weights(positions[0])
-        load_x(1)
-        for l in positions[1:HALF]:
-            load_weights(l)
-        load_scales(1)
-        for l in positions[HALF:]:
-            load_weights(l)
-
-        def quantise_x(half):
-            for m in range(B_TILES):
-                grouped = stage.tile([P, HALF, P, PACK], BF16, align_bytes=64)
-                for pair in range(HALF // 2):
-                    xt = psum_tr.tile([P, 2, 2, P], F32, tag="tr")
-                    for li in range(2):
-                        words = x_sb[:, m, HALF * half + 2 * pair + li, :].bitcast(F32)
-                        for u in range(2):
-                            nc.tensor.transpose(xt[:, li, u, :], words[:, u : C // 2 : 2], ident[:])
-                    nc.scalar.copy(
-                        out=grouped[:].bitcast(F32)[:, 2 * pair : 2 * pair + 2, :, :],
-                        in_=xt[:].rearrange("p l u b -> p l b u"),
-                    )
-                ls = slice(HALF * half, HALF * (half + 1))
-                nc.vector.quantize_mx(
-                    out=x_codes[:, m, ls, :].rearrange("p l b -> p (l b)").bitcast(FP8X4),
-                    scales=x_scales[:, m, ls, :].rearrange("p l b -> p (l b)"),
-                    in_=grouped[:].rearrange("p l b t -> p (l b t)"),
-                )
-
-        quantise_x(0)
+        x_pieces = [(m, half) for m in range(B_TILES) for half in range(2)]
+        for m, half in x_pieces:
+            ls = slice(HALF * half, HALF * (half + 1))
+            nc.sync.dma_start(out=x_sb[:, m, ls, :], in_=x_view[:, m, ls, :])
+        for half in range(2):
+            load_scales(half)
+            for l in range(HALF * half, HALF * (half + 1)):
+                for i in range(TAPS):
+                    nc.sync.dma_start(out=w_codes[:, l, i, :].bitcast(I32), in_=w_view[l, i].bitcast(I32))
 
         nc.vector.tensor_copy(out=raw[:], in_=raw_bf[:])
         cols_ps = psum_tr.tile([P, F_TILES, P], F32, tag="tr")
@@ -143,6 +113,38 @@ def tile_residualblock5_pa_t_e_kernel(tc, x, k1_words, k1_scales, b1, gamma1, be
             out=spread[:, :, 0:L], in0=spread[:, :, 0:L], in1=cols[:, :, ROW_BETA : ROW_BETA + 1].to_broadcast(per_position)
         )
 
+        def transpose_x(m, half):
+            grouped = stage.tile([P, HALF, P, PACK], BF16, align_bytes=64)
+            for pair in range(HALF // 2):
+                xt = psum_tr.tile([P, 2, 2, P], F32, tag="tr")
+                for li in range(2):
+                    words = x_sb[:, m, HALF * half + 2 * pair + li, :].bitcast(F32)
+                    for u in range(2):
+                        nc.tensor.transpose(xt[:, li, u, :], words[:, u : C // 2 : 2], ident[:])
+                target = grouped[:].bitcast(F32)[:, 2 * pair : 2 * pair + 2, :, :]
+                source = xt[:].rearrange("p l u b -> p l b u")
+                if pair == 0:
+                    nc.scalar.copy(out=target, in_=source)
+                else:
+                    nc.vector.tensor_copy(out=target, in_=source)
+            return grouped
+
+        def quantise_x(m, half, grouped):
+            ls = slice(HALF * half, HALF * (half + 1))
+            nc.vector.quantize_mx(
+                out=x_codes[:, m, ls, :].rearrange("p l b -> p (l b)").bitcast(FP8X4),
+                scales=x_scales[:, m, ls, :].rearrange("p l b -> p (l b)"),
+                in_=grouped[:].rearrange("p l b t -> p (l b t)"),
+            )
+
+        waiting = None
+        for m, half in x_pieces:
+            grouped = transpose_x(m, half)
+            if waiting is not None:
+                quantise_x(*waiting)
+            waiting = (m, half, grouped)
+        quantise_x(*waiting)
+
         def spread_row(r):
             row_ps = psum_tr.tile([P, F_TILES, P], F32, tag="tr")
             for j in range(F_TILES):
@@ -151,35 +153,35 @@ def tile_residualblock5_pa_t_e_kernel(tc, x, k1_words, k1_scales, b1, gamma1, be
 
         nc.vector.tensor_copy(out=gain_bc[:], in_=spread_row(GAIN))
 
-        def position(l):
+        def finish(l, m, z, shift_ps):
+            nc.vector.tensor_tensor(out=z[:], in0=z[:], in1=shift_ps, op=ALU.add)
+            lift = scratch.tile([P, F], F32)
+            nc.scalar.activation(out=lift[:], in_=z[:], func=ACT.Relu, scale=LEAKY_ALPHA - 1.0)
+            nc.gpsimd.tensor_tensor(out=z[:], in0=z[:], in1=lift[:], op=ALU.add)
+            nc.sync.dma_start(out=out_view[:, m, l, :], in_=z[:])
+
+        unfinished = None
+        for l in range(L):
             shift_ps = spread_row(l)
             first_row = PACK * (l % HALF)
             for pair in range(B_TILES // 2):
-                z = results.tile([P, 2, F], F32)
-                for k in range(2):
-                    m = 2 * pair + k
-                    acc = psum_acc.tile([P, F], F32)
-                    for i in range(TAPS):
-                        src = (l - TAP_STEP[i]) % L
+                banks = [psum_acc.tile([P, F], F32, name="acc") for k in range(2)]
+                for i in range(TAPS):
+                    src = (l - TAP_STEP[i]) % L
+                    for k in range(2):
                         nc.tensor.matmul_mx(
-                            out=acc[:],
-                            lhsT=x_codes[:, m, src, :].bitcast(FP8X4),
-                            lhsT_scale=x_scales[:, m, src, :],
+                            out=banks[k][:],
+                            lhsT=x_codes[:, 2 * pair + k, src, :].bitcast(FP8X4),
+                            lhsT_scale=x_scales[:, 2 * pair + k, src, :],
                             rhs=w_codes[:, l, i, :].bitcast(FP8X4),
                             rhs_scale=w_scales[first_row:P, l // HALF, i, :],
                             start=(i == 0),
                             stop=(i == TAPS - 1),
                         )
-                    nc.vector.tensor_tensor(out=z[:, k, :], in0=acc[:], in1=gain_bc[:], op=ALU.mult)
-                nc.vector.tensor_tensor(
-                    out=z[:], in0=z[:], in1=shift_ps.unsqueeze(1).to_broadcast([P, 2, F]), op=ALU.add
-                )
-                lift = scratch.tile([P, 2, F], F32)
-                nc.scalar.activation(out=lift[:], in_=z[:], func=ACT.Relu, scale=LEAKY_ALPHA - 1.0)
-                nc.gpsimd.tensor_tensor(out=z[:], in0=z[:], in1=lift[:], op=ALU.add)
-                nc.sync.dma_start(out=out_view[:, 2 * pair : 2 * pair + 2, l, :], in_=z[:])
-
-        position(positions[0])
-        quantise_x(1)
-        for l in positions[1:]:
-            position(l)
+                for k in range(2):
+                    z = results.tile([P, F], F32)
+                    nc.vector.tensor_tensor(out=z[:], in0=banks[k][:], in1=gain_bc[:], op=ALU.mult)
+                    if unfinished is not None:
+                        finish(*unfinished)
+                    unfinished = (l, 2 * pair + k, z, shift_ps)
+        finish(*unfinished)

@@ -35,7 +35,7 @@ def tile_residualblock5_pa_t_e_kernel(tc, x, k1_words, k1_scales, b1, gamma1, be
     with ExitStack() as ctx:
         ctx.enter_context(tc.manual_schedule())
         keep = ctx.enter_context(tc.tile_pool(name="keep", bufs=1))
-        stage = ctx.enter_context(tc.tile_pool(name="stage", bufs=3))
+        stage = ctx.enter_context(tc.tile_pool(name="stage", bufs=2))
         results = ctx.enter_context(tc.tile_pool(name="results", bufs=20))
         scratch = ctx.enter_context(tc.tile_pool(name="scratch", bufs=3))
         psum_tr = ctx.enter_context(tc.psum_pool(name="psum_tr", bufs=3))
@@ -45,7 +45,7 @@ def tile_residualblock5_pa_t_e_kernel(tc, x, k1_words, k1_scales, b1, gamma1, be
         x_codes = keep.tile([P, B_TILES, L, P], U32, align_bytes=64)
         x_scales = keep.tile([P, B_TILES, L, P], U8, align_bytes=64)
         w_codes = keep.tile([P, L, TAPS, F], U32, align_bytes=64)
-        w_scales = keep.tile([P, 2, TAPS, F], U8, align_bytes=64)
+        w_scales = keep.tile([P, TAPS, 2, F], U8, align_bytes=64)
         ident = keep.tile([P, P], F32)
         raw_bf = keep.tile([P, F], BF16)
         raw = keep.tile([P, F], F32)
@@ -56,9 +56,11 @@ def tile_residualblock5_pa_t_e_kernel(tc, x, k1_words, k1_scales, b1, gamma1, be
         spread = keep.tile([P, F_TILES, L + 1], F32)
         gain_bc = keep.tile([P, F], F32)
 
-        nc.vector.memset(w_scales[:].rearrange("p h i n -> p (h i n)").bitcast(I32), 0)
         nc.vector.memset(raw_bf[:], 0.0)
+        nc.vector.memset(var_eps[:], 1.0)
+        nc.vector.memset(w_scales[:].rearrange("p i h n -> p (i h n)").bitcast(I32), 0)
         make_identity(nc, ident[:])
+        nc.scalar.sqrt(out=std[:], in_=var_eps[:])
 
         nc.scalar.dma_start(out=raw_bf[0:L, :], in_=b1)
         for row, vec in ((ROW_GAMMA, gamma1), (ROW_BETA, beta1), (ROW_MEAN, mean1), (ROW_VAR, var1)):
@@ -66,84 +68,75 @@ def tile_residualblock5_pa_t_e_kernel(tc, x, k1_words, k1_scales, b1, gamma1, be
 
         x_view = x.rearrange("(m p) l c -> p m l c", p=P)
         w_view = k1_words.rearrange("(i l) p n t -> l i p (n t)", l=L)
-        s_view = k1_scales.rearrange("(i h j) q n -> h q j i n", h=2, j=HALF)
+        s_view = k1_scales.rearrange("(a j) (quad r) n -> j r quad a n", j=HALF, r=4)
         out_view = out.rearrange("(m p) l f -> p m l f", p=P)
 
-        def load_scales(half):
-            for quad in range(4):
-                for r in range(4):
-                    first = 32 * quad + r
-                    nc.sync.dma_start(
-                        out=w_scales[first : first + 16 : 4, half, :, :].bitcast(I32),
-                        in_=s_view[half, 4 * quad + r].bitcast(I32),
-                    )
+        for j in range(HALF):
+            for r in range(4):
+                nc.gpsimd.dma_start(
+                    out=w_scales[4 * j + r : P : 32, :, :, :].rearrange("q i h n -> q (i h) n").bitcast(F32),
+                    in_=s_view[j, r].bitcast(F32),
+                )
 
-        x_pieces = [(m, half) for m in range(B_TILES) for half in range(2)]
-        for m, half in x_pieces:
-            ls = slice(HALF * half, HALF * (half + 1))
-            nc.sync.dma_start(out=x_sb[:, m, ls, :], in_=x_view[:, m, ls, :])
-        for half in range(2):
-            load_scales(half)
-            for l in range(HALF * half, HALF * (half + 1)):
-                for i in range(TAPS):
-                    nc.sync.dma_start(out=w_codes[:, l, i, :].bitcast(I32), in_=w_view[l, i].bitcast(I32))
+        for m in range(B_TILES):
+            for half in range(2):
+                ls = slice(HALF * half, HALF * (half + 1))
+                nc.sync.dma_start(out=x_sb[:, m, ls, :], in_=x_view[:, m, ls, :])
+        for l in range(L):
+            for i in range(TAPS):
+                nc.sync.dma_start(out=w_codes[:, l, i, :].bitcast(I32), in_=w_view[l, i].bitcast(I32))
 
-        nc.vector.tensor_copy(out=raw[:], in_=raw_bf[:])
-        cols_ps = psum_tr.tile([P, F_TILES, P], F32, tag="tr")
-        for j in range(F_TILES):
-            nc.tensor.transpose(cols_ps[:, j, :], raw[:, j * P : (j + 1) * P], ident[:])
-        nc.vector.tensor_copy(out=cols[:], in_=cols_ps[:, :, 0:ROWS])
-        nc.vector.tensor_scalar_add(out=var_eps[:], in0=cols[:, :, ROW_VAR], scalar1=BN_EPS)
-        nc.scalar.sqrt(out=std[:], in_=var_eps[:])
-        nc.vector.reciprocal(out=rstd[:], in_=std[:])
-        nc.vector.tensor_mul(out=spread[:, :, GAIN], in0=cols[:, :, ROW_GAMMA], in1=rstd[:])
-        per_position = [P, F_TILES, L]
-        nc.vector.scalar_tensor_tensor(
-            out=spread[:, :, 0:L],
-            in0=cols[:, :, 0:L],
-            scalar=2.0,
-            in1=cols[:, :, ROW_MEAN : ROW_MEAN + 1].to_broadcast(per_position),
-            op0=ALU.mult,
-            op1=ALU.subtract,
-        )
-        nc.vector.tensor_mul(
-            out=spread[:, :, 0:L], in0=spread[:, :, 0:L], in1=spread[:, :, GAIN : GAIN + 1].to_broadcast(per_position)
-        )
-        nc.vector.tensor_add(
-            out=spread[:, :, 0:L], in0=spread[:, :, 0:L], in1=cols[:, :, ROW_BETA : ROW_BETA + 1].to_broadcast(per_position)
-        )
-
-        def transpose_x(m, half):
-            grouped = stage.tile([P, HALF, P, PACK], BF16, align_bytes=64)
-            for pair in range(HALF // 2):
+        def quantise_x(m):
+            grouped = stage.tile([P, L, P, PACK], BF16, align_bytes=64)
+            for pair in range(L // 2):
                 xt = psum_tr.tile([P, 2, 2, P], F32, tag="tr")
                 for li in range(2):
-                    words = x_sb[:, m, HALF * half + 2 * pair + li, :].bitcast(F32)
+                    words = x_sb[:, m, 2 * pair + li, :].bitcast(F32)
                     for u in range(2):
                         nc.tensor.transpose(xt[:, li, u, :], words[:, u : C // 2 : 2], ident[:])
                 target = grouped[:].bitcast(F32)[:, 2 * pair : 2 * pair + 2, :, :]
                 source = xt[:].rearrange("p l u b -> p l b u")
-                if pair == 0:
+                if pair % 2 == 0:
                     nc.scalar.copy(out=target, in_=source)
                 else:
                     nc.vector.tensor_copy(out=target, in_=source)
-            return grouped
-
-        def quantise_x(m, half, grouped):
-            ls = slice(HALF * half, HALF * (half + 1))
             nc.vector.quantize_mx(
-                out=x_codes[:, m, ls, :].rearrange("p l b -> p (l b)").bitcast(FP8X4),
-                scales=x_scales[:, m, ls, :].rearrange("p l b -> p (l b)"),
+                out=x_codes[:, m, :, :].rearrange("p l b -> p (l b)").bitcast(FP8X4),
+                scales=x_scales[:, m, :, :].rearrange("p l b -> p (l b)"),
                 in_=grouped[:].rearrange("p l b t -> p (l b t)"),
             )
 
-        waiting = None
-        for m, half in x_pieces:
-            grouped = transpose_x(m, half)
-            if waiting is not None:
-                quantise_x(*waiting)
-            waiting = (m, half, grouped)
-        quantise_x(*waiting)
+        def vectors_to_columns():
+            nc.vector.tensor_copy(out=raw[:], in_=raw_bf[:])
+            cols_ps = psum_tr.tile([P, F_TILES, P], F32, tag="tr")
+            for j in range(F_TILES):
+                nc.tensor.transpose(cols_ps[:, j, :], raw[:, j * P : (j + 1) * P], ident[:])
+            nc.vector.tensor_copy(out=cols[:], in_=cols_ps[:, :, 0:ROWS])
+            nc.vector.tensor_scalar_add(out=var_eps[:], in0=cols[:, :, ROW_VAR], scalar1=BN_EPS)
+            nc.scalar.sqrt(out=std[:], in_=var_eps[:])
+
+        def gain_and_shift():
+            per_position = [P, F_TILES, L]
+            nc.vector.reciprocal(out=rstd[:], in_=std[:])
+            nc.vector.tensor_mul(out=spread[:, :, GAIN], in0=cols[:, :, ROW_GAMMA], in1=rstd[:])
+            nc.vector.scalar_tensor_tensor(
+                out=spread[:, :, 0:L],
+                in0=cols[:, :, 0:L],
+                scalar=2.0,
+                in1=cols[:, :, ROW_MEAN : ROW_MEAN + 1].to_broadcast(per_position),
+                op0=ALU.mult,
+                op1=ALU.subtract,
+            )
+            nc.vector.tensor_mul(
+                out=spread[:, :, 0:L],
+                in0=spread[:, :, 0:L],
+                in1=spread[:, :, GAIN : GAIN + 1].to_broadcast(per_position),
+            )
+            nc.vector.tensor_add(
+                out=spread[:, :, 0:L],
+                in0=spread[:, :, 0:L],
+                in1=cols[:, :, ROW_BETA : ROW_BETA + 1].to_broadcast(per_position),
+            )
 
         def spread_row(r):
             row_ps = psum_tr.tile([P, F_TILES, P], F32, tag="tr")
@@ -151,6 +144,12 @@ def tile_residualblock5_pa_t_e_kernel(tc, x, k1_words, k1_scales, b1, gamma1, be
                 nc.tensor.transpose(row_ps[:, j, :], spread[:, j, r : r + 1].to_broadcast([P, P]), ident[:])
             return row_ps[:].rearrange("p j n -> p (j n)")
 
+        quantise_x(0)
+        vectors_to_columns()
+        quantise_x(1)
+        gain_and_shift()
+        quantise_x(2)
+        quantise_x(3)
         nc.vector.tensor_copy(out=gain_bc[:], in_=spread_row(GAIN))
 
         def finish(l, m, z, shift_ps):
@@ -174,7 +173,7 @@ def tile_residualblock5_pa_t_e_kernel(tc, x, k1_words, k1_scales, b1, gamma1, be
                             lhsT=x_codes[:, 2 * pair + k, src, :].bitcast(FP8X4),
                             lhsT_scale=x_scales[:, 2 * pair + k, src, :],
                             rhs=w_codes[:, l, i, :].bitcast(FP8X4),
-                            rhs_scale=w_scales[first_row:P, l // HALF, i, :],
+                            rhs_scale=w_scales[first_row:P, i, l // HALF, :],
                             start=(i == 0),
                             stop=(i == TAPS - 1),
                         )

@@ -36,7 +36,7 @@ def tile_residualblock5_pa_t_e_kernel(tc, x, k1_words, k1_scales, b1, gamma1, be
         ctx.enter_context(tc.manual_schedule())
         keep = ctx.enter_context(tc.tile_pool(name="keep", bufs=1))
         stage = ctx.enter_context(tc.tile_pool(name="stage", bufs=2))
-        results = ctx.enter_context(tc.tile_pool(name="results", bufs=20))
+        results = ctx.enter_context(tc.tile_pool(name="results", bufs=16))
         scratch = ctx.enter_context(tc.tile_pool(name="scratch", bufs=3))
         psum_tr = ctx.enter_context(tc.psum_pool(name="psum_tr", bufs=3))
         psum_acc = ctx.enter_context(tc.psum_pool(name="psum_acc", bufs=5))
@@ -45,7 +45,7 @@ def tile_residualblock5_pa_t_e_kernel(tc, x, k1_words, k1_scales, b1, gamma1, be
         x_codes = keep.tile([P, B_TILES, L, P], U32, align_bytes=64)
         x_scales = keep.tile([P, B_TILES, L, P], U8, align_bytes=64)
         w_codes = keep.tile([P, L, TAPS, F], U32, align_bytes=64)
-        w_scales = keep.tile([P, TAPS, 2, F], U8, align_bytes=64)
+        w_scales = keep.tile([P, TAPS * L, F], U8, align_bytes=64)
         ident = keep.tile([P, P], F32)
         raw_bf = keep.tile([P, F], BF16)
         raw = keep.tile([P, F], F32)
@@ -58,7 +58,7 @@ def tile_residualblock5_pa_t_e_kernel(tc, x, k1_words, k1_scales, b1, gamma1, be
 
         nc.vector.memset(raw_bf[:], 0.0)
         nc.vector.memset(var_eps[:], 1.0)
-        nc.vector.memset(w_scales[:].rearrange("p i h n -> p (i h n)").bitcast(I32), 0)
+        nc.vector.memset(w_scales[:].rearrange("p g n -> p (g n)").bitcast(I32), 0)
         make_identity(nc, ident[:])
         nc.scalar.sqrt(out=std[:], in_=var_eps[:])
 
@@ -68,15 +68,11 @@ def tile_residualblock5_pa_t_e_kernel(tc, x, k1_words, k1_scales, b1, gamma1, be
 
         x_view = x.rearrange("(m p) l c -> p m l c", p=P)
         w_view = k1_words.rearrange("(i l) p n t -> l i p (n t)", l=L)
-        s_view = k1_scales.rearrange("(a j) (quad r) n -> j r quad a n", j=HALF, r=4)
+        s_view = k1_scales.rearrange("g (quad r) n -> r quad g n", r=4)
         out_view = out.rearrange("(m p) l f -> p m l f", p=P)
 
-        for j in range(HALF):
-            for r in range(4):
-                nc.gpsimd.dma_start(
-                    out=w_scales[4 * j + r : P : 32, :, :, :].rearrange("q i h n -> q (i h) n").bitcast(F32),
-                    in_=s_view[j, r].bitcast(F32),
-                )
+        for r in range(4):
+            nc.gpsimd.dma_start(out=w_scales[r:P:32, :, :].bitcast(F32), in_=s_view[r].bitcast(F32))
 
         for m in range(B_TILES):
             for half in range(2):
@@ -162,7 +158,6 @@ def tile_residualblock5_pa_t_e_kernel(tc, x, k1_words, k1_scales, b1, gamma1, be
         unfinished = None
         for l in range(L):
             shift_ps = spread_row(l)
-            first_row = PACK * (l % HALF)
             for pair in range(B_TILES // 2):
                 banks = [psum_acc.tile([P, F], F32, name="acc") for k in range(2)]
                 for i in range(TAPS):
@@ -173,7 +168,7 @@ def tile_residualblock5_pa_t_e_kernel(tc, x, k1_words, k1_scales, b1, gamma1, be
                             lhsT=x_codes[:, 2 * pair + k, src, :].bitcast(FP8X4),
                             lhsT_scale=x_scales[:, 2 * pair + k, src, :],
                             rhs=w_codes[:, l, i, :].bitcast(FP8X4),
-                            rhs_scale=w_scales[first_row:P, i, l // HALF, :],
+                            rhs_scale=w_scales[:, L * i + l, :],
                             start=(i == 0),
                             stop=(i == TAPS - 1),
                         )

@@ -19,7 +19,7 @@ TAP_STEP = (0, 0, 1, -1, 2)
 TAPS = len(TAP_STEP)
 B_TILES = B // P
 F_TILES = F // P
-HALF = L // 2
+PAIRS = L // 2
 BN_EPS = 1e-3
 LEAKY_ALPHA = 0.3
 
@@ -35,16 +35,18 @@ def tile_residualblock5_pa_t_e_kernel(tc, x, k1_words, k1_scales, b1, gamma1, be
     with ExitStack() as ctx:
         ctx.enter_context(tc.manual_schedule())
         keep = ctx.enter_context(tc.tile_pool(name="keep", bufs=1))
-        stage = ctx.enter_context(tc.tile_pool(name="stage", bufs=2))
-        results = ctx.enter_context(tc.tile_pool(name="results", bufs=16))
+        stage = ctx.enter_context(tc.tile_pool(name="stage", bufs=4))
+        results = ctx.enter_context(tc.tile_pool(name="results", bufs=12))
         scratch = ctx.enter_context(tc.tile_pool(name="scratch", bufs=3))
-        psum_tr = ctx.enter_context(tc.psum_pool(name="psum_tr", bufs=3))
-        psum_acc = ctx.enter_context(tc.psum_pool(name="psum_acc", bufs=5))
+        psum_xt = ctx.enter_context(tc.psum_pool(name="psum_xt", bufs=2))
+        psum_row = ctx.enter_context(tc.psum_pool(name="psum_row", bufs=2))
+        psum_acc = ctx.enter_context(tc.psum_pool(name="psum_acc", bufs=4))
 
         x_sb = keep.tile([P, B_TILES, L, C], BF16)
         x_codes = keep.tile([P, B_TILES, L, P], U32, align_bytes=64)
         x_scales = keep.tile([P, B_TILES, L, P], U8, align_bytes=64)
         w_codes = keep.tile([P, L, TAPS, F], U32, align_bytes=64)
+        w_scales_first = keep.tile([P, TAPS, F], U8, align_bytes=64)
         w_scales = keep.tile([P, TAPS * L, F], U8, align_bytes=64)
         ident = keep.tile([P, P], F32)
         raw_bf = keep.tile([P, F], BF16)
@@ -58,6 +60,7 @@ def tile_residualblock5_pa_t_e_kernel(tc, x, k1_words, k1_scales, b1, gamma1, be
 
         nc.vector.memset(raw_bf[:], 0.0)
         nc.vector.memset(var_eps[:], 1.0)
+        nc.vector.memset(w_scales_first[:].rearrange("p g n -> p (g n)").bitcast(I32), 0)
         nc.vector.memset(w_scales[:].rearrange("p g n -> p (g n)").bitcast(I32), 0)
         make_identity(nc, ident[:])
         nc.scalar.sqrt(out=std[:], in_=var_eps[:])
@@ -67,44 +70,61 @@ def tile_residualblock5_pa_t_e_kernel(tc, x, k1_words, k1_scales, b1, gamma1, be
             nc.scalar.dma_start(out=raw_bf[row : row + 1, :], in_=vec.unsqueeze(0))
 
         x_view = x.rearrange("(m p) l c -> p m l c", p=P)
-        w_view = k1_words.rearrange("(i l) p n t -> l i p (n t)", l=L)
+        w_view = k1_words.rearrange("(i l) p n t -> l p i (n t)", l=L)
         s_view = k1_scales.rearrange("g (quad r) n -> r quad g n", r=4)
         out_view = out.rearrange("(m p) l f -> p m l f", p=P)
 
         for r in range(4):
+            nc.gpsimd.dma_start(out=w_scales_first[r:P:32, :, :].bitcast(F32), in_=s_view[r][:, 0 : TAPS * L : L, :].bitcast(F32))
+        for r in range(4):
             nc.gpsimd.dma_start(out=w_scales[r:P:32, :, :].bitcast(F32), in_=s_view[r].bitcast(F32))
 
-        for m in range(B_TILES):
-            for half in range(2):
-                ls = slice(HALF * half, HALF * (half + 1))
+        def load_x(pair, m=None):
+            ls = slice(2 * pair, 2 * pair + 2)
+            if m is None:
+                nc.sync.dma_start(out=x_sb[:, :, ls, :], in_=x_view[:, :, ls, :])
+            else:
                 nc.sync.dma_start(out=x_sb[:, m, ls, :], in_=x_view[:, m, ls, :])
-        for l in range(L):
-            for i in range(TAPS):
-                nc.sync.dma_start(out=w_codes[:, l, i, :].bitcast(I32), in_=w_view[l, i].bitcast(I32))
 
-        def quantise_x(m):
-            grouped = stage.tile([P, L, P, PACK], BF16, align_bytes=64)
-            for pair in range(L // 2):
-                xt = psum_tr.tile([P, 2, 2, P], F32, tag="tr")
-                for li in range(2):
-                    words = x_sb[:, m, 2 * pair + li, :].bitcast(F32)
-                    for u in range(2):
-                        nc.tensor.transpose(xt[:, li, u, :], words[:, u : C // 2 : 2], ident[:])
-                target = grouped[:].bitcast(F32)[:, 2 * pair : 2 * pair + 2, :, :]
-                source = xt[:].rearrange("p l u b -> p l b u")
-                if pair % 2 == 0:
-                    nc.scalar.copy(out=target, in_=source)
-                else:
-                    nc.vector.tensor_copy(out=target, in_=source)
+        def load_w(l, taps=slice(0, TAPS)):
+            nc.sync.dma_start(out=w_codes[:, l, taps, :].bitcast(I32), in_=w_view[l][:, taps, :].bitcast(I32))
+
+        FIRST_TAPS = (0, 1, 3, 2, 4)
+        LATER_TAPS = (0, 1, 2, 4, 3)
+        AHEAD = 4
+
+        for pair in (0, PAIRS - 1):
+            for m in range(B_TILES):
+                load_x(pair, m)
+        for i in FIRST_TAPS:
+            load_w(0, slice(i, i + 1))
+        load_x(1)
+        load_w(1)
+        load_x(2)
+        load_w(2)
+        load_w(3)
+
+        def transpose_chunk(m, pair, copy):
+            xt = psum_xt.tile([P, 2, 2, P], F32, tag="xt")
+            for li in range(2):
+                words = x_sb[:, m, 2 * pair + li, :].bitcast(F32)
+                for u in range(2):
+                    nc.tensor.transpose(xt[:, li, u, :], words[:, u : C // 2 : 2], ident[:])
+            grouped = stage.tile([P, 2, P, PACK], BF16, align_bytes=64)
+            copy(out=grouped[:].bitcast(F32), in_=xt[:].rearrange("p l u b -> p l b u"))
+            return (m, pair, grouped)
+
+        def quantise_chunk(m, pair, grouped):
+            ls = slice(2 * pair, 2 * pair + 2)
             nc.vector.quantize_mx(
-                out=x_codes[:, m, :, :].rearrange("p l b -> p (l b)").bitcast(FP8X4),
-                scales=x_scales[:, m, :, :].rearrange("p l b -> p (l b)"),
+                out=x_codes[:, m, ls, :].rearrange("p l b -> p (l b)").bitcast(FP8X4),
+                scales=x_scales[:, m, ls, :].rearrange("p l b -> p (l b)"),
                 in_=grouped[:].rearrange("p l b t -> p (l b t)"),
             )
 
         def vectors_to_columns():
             nc.vector.tensor_copy(out=raw[:], in_=raw_bf[:])
-            cols_ps = psum_tr.tile([P, F_TILES, P], F32, tag="tr")
+            cols_ps = psum_xt.tile([P, F_TILES, P], F32, tag="xt")
             for j in range(F_TILES):
                 nc.tensor.transpose(cols_ps[:, j, :], raw[:, j * P : (j + 1) * P], ident[:])
             nc.vector.tensor_copy(out=cols[:], in_=cols_ps[:, :, 0:ROWS])
@@ -135,18 +155,41 @@ def tile_residualblock5_pa_t_e_kernel(tc, x, k1_words, k1_scales, b1, gamma1, be
             )
 
         def spread_row(r):
-            row_ps = psum_tr.tile([P, F_TILES, P], F32, tag="tr")
+            row_ps = psum_row.tile([P, F_TILES, P], F32, tag="row")
             for j in range(F_TILES):
                 nc.tensor.transpose(row_ps[:, j, :], spread[:, j, r : r + 1].to_broadcast([P, P]), ident[:])
             return row_ps[:].rearrange("p j n -> p (j n)")
 
-        quantise_x(0)
+        waiting = []
+        quantised = [0]
+
+        def quantise_next():
+            quantise_chunk(*waiting[quantised[0]])
+            quantised[0] += 1
+
         vectors_to_columns()
-        quantise_x(1)
-        gain_and_shift()
-        quantise_x(2)
-        quantise_x(3)
-        nc.vector.tensor_copy(out=gain_bc[:], in_=spread_row(GAIN))
+        head = [(m, pair) for pair in (0, PAIRS - 1) for m in range(B_TILES)]
+        for n, (m, pair) in enumerate(head):
+            waiting.append(transpose_chunk(m, pair, nc.scalar.copy if n % 2 == 0 else nc.vector.tensor_copy))
+            if n >= 1:
+                quantise_next()
+            if n == 1:
+                gain_and_shift()
+            if n == 5:
+                nc.scalar.copy(out=gain_bc[:], in_=spread_row(GAIN))
+        quantise_next()
+
+        def product(bank, l, m, i, taps):
+            src = (l - TAP_STEP[i]) % L
+            nc.tensor.matmul_mx(
+                out=bank[:],
+                lhsT=x_codes[:, m, src, :].bitcast(FP8X4),
+                lhsT_scale=x_scales[:, m, src, :],
+                rhs=w_codes[:, l, i, :].bitcast(FP8X4),
+                rhs_scale=w_scales_first[:, i, :] if l == 0 else w_scales[:, L * i + l, :],
+                start=(i == taps[0]),
+                stop=(i == taps[-1]),
+            )
 
         def finish(l, m, z, shift_ps):
             nc.vector.tensor_tensor(out=z[:], in0=z[:], in1=shift_ps, op=ALU.add)
@@ -154,28 +197,45 @@ def tile_residualblock5_pa_t_e_kernel(tc, x, k1_words, k1_scales, b1, gamma1, be
             nc.scalar.activation(out=lift[:], in_=z[:], func=ACT.Relu, scale=LEAKY_ALPHA - 1.0)
             nc.gpsimd.tensor_tensor(out=z[:], in0=z[:], in1=lift[:], op=ALU.add)
             nc.sync.dma_start(out=out_view[:, m, l, :], in_=z[:])
+            if m == B_TILES - 1 and l + AHEAD < L:
+                load_w(l + AHEAD)
 
-        unfinished = None
-        for l in range(L):
-            shift_ps = spread_row(l)
-            for pair in range(B_TILES // 2):
-                banks = [psum_acc.tile([P, F], F32, name="acc") for k in range(2)]
-                for i in range(TAPS):
-                    src = (l - TAP_STEP[i]) % L
-                    for k in range(2):
-                        nc.tensor.matmul_mx(
-                            out=banks[k][:],
-                            lhsT=x_codes[:, 2 * pair + k, src, :].bitcast(FP8X4),
-                            lhsT_scale=x_scales[:, 2 * pair + k, src, :],
-                            rhs=w_codes[:, l, i, :].bitcast(FP8X4),
-                            rhs_scale=w_scales[:, L * i + l, :],
-                            start=(i == 0),
-                            stop=(i == TAPS - 1),
-                        )
-                for k in range(2):
-                    z = results.tile([P, F], F32)
-                    nc.vector.tensor_tensor(out=z[:], in0=banks[k][:], in1=gain_bc[:], op=ALU.mult)
-                    if unfinished is not None:
-                        finish(*unfinished)
-                    unfinished = (l, 2 * pair + k, z, shift_ps)
-        finish(*unfinished)
+        emptied = []
+
+        def empty(bank, l, m, shift_ps):
+            z = results.tile([P, F], F32)
+            nc.vector.tensor_tensor(out=z[:], in0=bank[:], in1=gain_bc[:], op=ALU.mult)
+            if emptied:
+                finish(*emptied[-1])
+            emptied.append((l, m, z, shift_ps))
+
+        def prepare(l):
+            if l in (1, 2):
+                for m in range(B_TILES):
+                    waiting.append(transpose_chunk(m, l, nc.scalar.copy))
+            return spread_row(l)
+
+        shift_ps = prepare(0)
+        banks = [psum_acc.tile([P, F], F32, name="acc") for m in range(B_TILES)]
+        for i in FIRST_TAPS:
+            for m in range(B_TILES):
+                product(banks[m], 0, m, i, FIRST_TAPS)
+        next_shift = prepare(1)
+        for m in range(B_TILES):
+            empty(banks[m], 0, m, shift_ps)
+            if m >= 1:
+                quantise_next()
+        quantise_next()
+
+        for l in range(1, L):
+            shift_ps = next_shift
+            for m in range(B_TILES):
+                bank = psum_acc.tile([P, F], F32, name="acc")
+                for i in LATER_TAPS:
+                    product(bank, l, m, i, LATER_TAPS)
+                empty(bank, l, m, shift_ps)
+                if quantised[0] < len(waiting):
+                    quantise_next()
+            if l + 1 < L:
+                next_shift = prepare(l + 1)
+        finish(*emptied[-1])

@@ -36,7 +36,7 @@ def tile_residualblock5_pa_t_e_kernel(tc, x, k1_words, k1_scales, b1, gamma1, be
         ctx.enter_context(tc.manual_schedule())
         keep = ctx.enter_context(tc.tile_pool(name="keep", bufs=1))
         stage = ctx.enter_context(tc.tile_pool(name="stage", bufs=4))
-        results = ctx.enter_context(tc.tile_pool(name="results", bufs=12))
+        results = ctx.enter_context(tc.tile_pool(name="results", bufs=16))
         scratch = ctx.enter_context(tc.tile_pool(name="scratch", bufs=3))
         psum_xt = ctx.enter_context(tc.psum_pool(name="psum_xt", bufs=2))
         psum_row = ctx.enter_context(tc.psum_pool(name="psum_row", bufs=2))
@@ -63,11 +63,11 @@ def tile_residualblock5_pa_t_e_kernel(tc, x, k1_words, k1_scales, b1, gamma1, be
         nc.vector.memset(w_scales_first[:].rearrange("p g n -> p (g n)").bitcast(I32), 0)
         nc.vector.memset(w_scales[:].rearrange("p g n -> p (g n)").bitcast(I32), 0)
         make_identity(nc, ident[:])
-        nc.scalar.sqrt(out=std[:], in_=var_eps[:])
 
         nc.scalar.dma_start(out=raw_bf[0:L, :], in_=b1)
         for row, vec in ((ROW_GAMMA, gamma1), (ROW_BETA, beta1), (ROW_MEAN, mean1), (ROW_VAR, var1)):
             nc.scalar.dma_start(out=raw_bf[row : row + 1, :], in_=vec.unsqueeze(0))
+        nc.scalar.sqrt(out=std[:], in_=var_eps[:])
 
         x_view = x.rearrange("(m p) l c -> p m l c", p=P)
         w_view = k1_words.rearrange("(i l) p n t -> l p i (n t)", l=L)
@@ -75,34 +75,30 @@ def tile_residualblock5_pa_t_e_kernel(tc, x, k1_words, k1_scales, b1, gamma1, be
         out_view = out.rearrange("(m p) l f -> p m l f", p=P)
 
         for r in range(4):
-            nc.gpsimd.dma_start(out=w_scales_first[r:P:32, :, :].bitcast(F32), in_=s_view[r][:, 0 : TAPS * L : L, :].bitcast(F32))
-        for r in range(4):
             nc.gpsimd.dma_start(out=w_scales[r:P:32, :, :].bitcast(F32), in_=s_view[r].bitcast(F32))
 
-        def load_x(pair, m=None):
+        def load_x(pair):
             ls = slice(2 * pair, 2 * pair + 2)
-            if m is None:
-                nc.sync.dma_start(out=x_sb[:, :, ls, :], in_=x_view[:, :, ls, :])
-            else:
-                nc.sync.dma_start(out=x_sb[:, m, ls, :], in_=x_view[:, m, ls, :])
+            for ms in (slice(0, 2), slice(2, 4)):
+                nc.sync.dma_start(out=x_sb[:, ms, ls, :], in_=x_view[:, ms, ls, :])
 
-        def load_w(l, taps=slice(0, TAPS)):
-            nc.sync.dma_start(out=w_codes[:, l, taps, :].bitcast(I32), in_=w_view[l][:, taps, :].bitcast(I32))
+        def load_w(l, taps):
+            for i in taps:
+                nc.sync.dma_start(out=w_codes[:, l, i, :].bitcast(I32), in_=w_view[l][:, i, :].bitcast(I32))
 
         FIRST_TAPS = (0, 1, 3, 2, 4)
         LATER_TAPS = (0, 1, 2, 4, 3)
-        AHEAD = 4
 
-        for pair in (0, PAIRS - 1):
-            for m in range(B_TILES):
-                load_x(pair, m)
-        for i in FIRST_TAPS:
-            load_w(0, slice(i, i + 1))
+        load_x(0)
+        load_x(PAIRS - 1)
+        for r in range(4):
+            nc.sync.dma_start(out=w_scales_first[r:P:32, :, :].bitcast(I32), in_=s_view[r][:, 0 : TAPS * L : L, :].bitcast(I32))
+        load_w(0, FIRST_TAPS)
         load_x(1)
-        load_w(1)
+        load_w(1, LATER_TAPS)
         load_x(2)
-        load_w(2)
-        load_w(3)
+        for l in range(2, L):
+            load_w(l, LATER_TAPS)
 
         def transpose_chunk(m, pair, copy):
             xt = psum_xt.tile([P, 2, 2, P], F32, tag="xt")
@@ -123,13 +119,11 @@ def tile_residualblock5_pa_t_e_kernel(tc, x, k1_words, k1_scales, b1, gamma1, be
             )
 
         def vectors_to_columns():
-            nc.vector.tensor_copy(out=raw[:], in_=raw_bf[:])
-            cols_ps = psum_xt.tile([P, F_TILES, P], F32, tag="xt")
+            cols_ps = psum_row.tile([P, F_TILES, P], F32, tag="row")
             for j in range(F_TILES):
                 nc.tensor.transpose(cols_ps[:, j, :], raw[:, j * P : (j + 1) * P], ident[:])
             nc.vector.tensor_copy(out=cols[:], in_=cols_ps[:, :, 0:ROWS])
             nc.vector.tensor_scalar_add(out=var_eps[:], in0=cols[:, :, ROW_VAR], scalar1=BN_EPS)
-            nc.scalar.sqrt(out=std[:], in_=var_eps[:])
 
         def gain_and_shift():
             per_position = [P, F_TILES, L]
@@ -167,13 +161,17 @@ def tile_residualblock5_pa_t_e_kernel(tc, x, k1_words, k1_scales, b1, gamma1, be
             quantise_chunk(*waiting[quantised[0]])
             quantised[0] += 1
 
-        vectors_to_columns()
+        nc.vector.tensor_copy(out=raw[:], in_=raw_bf[:])
         head = [(m, pair) for pair in (0, PAIRS - 1) for m in range(B_TILES)]
         for n, (m, pair) in enumerate(head):
             waiting.append(transpose_chunk(m, pair, nc.scalar.copy if n % 2 == 0 else nc.vector.tensor_copy))
             if n >= 1:
                 quantise_next()
             if n == 1:
+                vectors_to_columns()
+            if n == 2:
+                nc.scalar.sqrt(out=std[:], in_=var_eps[:])
+            if n == 3:
                 gain_and_shift()
             if n == 5:
                 nc.scalar.copy(out=gain_bc[:], in_=spread_row(GAIN))
@@ -197,8 +195,6 @@ def tile_residualblock5_pa_t_e_kernel(tc, x, k1_words, k1_scales, b1, gamma1, be
             nc.scalar.activation(out=lift[:], in_=z[:], func=ACT.Relu, scale=LEAKY_ALPHA - 1.0)
             nc.gpsimd.tensor_tensor(out=z[:], in0=z[:], in1=lift[:], op=ALU.add)
             nc.sync.dma_start(out=out_view[:, m, l, :], in_=z[:])
-            if m == B_TILES - 1 and l + AHEAD < L:
-                load_w(l + AHEAD)
 
         emptied = []
 
@@ -229,13 +225,15 @@ def tile_residualblock5_pa_t_e_kernel(tc, x, k1_words, k1_scales, b1, gamma1, be
 
         for l in range(1, L):
             shift_ps = next_shift
-            for m in range(B_TILES):
-                bank = psum_acc.tile([P, F], F32, name="acc")
+            for pair in range(B_TILES // 2):
+                banks = [psum_acc.tile([P, F], F32, name="acc") for k in range(2)]
                 for i in LATER_TAPS:
-                    product(bank, l, m, i, LATER_TAPS)
-                empty(bank, l, m, shift_ps)
-                if quantised[0] < len(waiting):
-                    quantise_next()
+                    for k in range(2):
+                        product(banks[k], l, 2 * pair + k, i, LATER_TAPS)
+                for k in range(2):
+                    empty(banks[k], l, 2 * pair + k, shift_ps)
+                    if quantised[0] < len(waiting):
+                        quantise_next()
             if l + 1 < L:
                 next_shift = prepare(l + 1)
         finish(*emptied[-1])

@@ -42,12 +42,11 @@ def tile_residualblock5_pa_t_e_kernel(tc, x, k1_words, k1_scales, b1, gamma1, be
         psum_row = ctx.enter_context(tc.psum_pool(name="psum_row", bufs=2))
         psum_acc = ctx.enter_context(tc.psum_pool(name="psum_acc", bufs=4))
 
-        x_sb = keep.tile([P, B_TILES, L, C], BF16)
+        x_sb = keep.tile([P, PAIRS, B_TILES, 2, C], BF16)
         x_codes = keep.tile([P, B_TILES, L, P], U32, align_bytes=64)
         x_scales = keep.tile([P, B_TILES, L, P], U8, align_bytes=64)
         w_codes = keep.tile([P, L, TAPS, F], U32, align_bytes=64)
-        w_scales_first = keep.tile([P, TAPS, F], U8, align_bytes=64)
-        w_scales = keep.tile([P, TAPS * L, F], U8, align_bytes=64)
+        w_scales = [keep.tile([P, TAPS, F], U8, align_bytes=64, name="w_scales_%d" % l) for l in range(L)]
         ident = keep.tile([P, P], F32)
         raw_bf = keep.tile([P, F], BF16)
         raw = keep.tile([P, F], F32)
@@ -60,8 +59,8 @@ def tile_residualblock5_pa_t_e_kernel(tc, x, k1_words, k1_scales, b1, gamma1, be
 
         nc.vector.memset(raw_bf[:], 0.0)
         nc.vector.memset(var_eps[:], 1.0)
-        nc.vector.memset(w_scales_first[:].rearrange("p g n -> p (g n)").bitcast(I32), 0)
-        nc.vector.memset(w_scales[:].rearrange("p g n -> p (g n)").bitcast(I32), 0)
+        for l in range(L):
+            nc.vector.memset(w_scales[l][:].rearrange("p i n -> p (i n)").bitcast(I32), 0)
         make_identity(nc, ident[:])
 
         nc.scalar.dma_start(out=raw_bf[0:L, :], in_=b1)
@@ -74,13 +73,17 @@ def tile_residualblock5_pa_t_e_kernel(tc, x, k1_words, k1_scales, b1, gamma1, be
         s_view = k1_scales.rearrange("g (quad r) n -> r quad g n", r=4)
         out_view = out.rearrange("(m p) l f -> p m l f", p=P)
 
-        for r in range(4):
-            nc.gpsimd.dma_start(out=w_scales[r:P:32, :, :].bitcast(F32), in_=s_view[r].bitcast(F32))
+        def load_x(pair, half):
+            nc.sync.dma_start(
+                out=x_sb[:, pair, 2 * half : 2 * half + 2, :, :],
+                in_=x_view[:, 2 * half : 2 * half + 2, 2 * pair : 2 * pair + 2, :],
+            )
 
-        def load_x(pair):
-            ls = slice(2 * pair, 2 * pair + 2)
-            for ms in (slice(0, 2), slice(2, 4)):
-                nc.sync.dma_start(out=x_sb[:, ms, ls, :], in_=x_view[:, ms, ls, :])
+        def load_scales(l):
+            for r in range(4):
+                nc.sync.dma_start(
+                    out=w_scales[l][r:P:32, :, :].bitcast(I32), in_=s_view[r][:, l : TAPS * L : L, :].bitcast(I32)
+                )
 
         def load_w(l, taps):
             for i in taps:
@@ -88,22 +91,27 @@ def tile_residualblock5_pa_t_e_kernel(tc, x, k1_words, k1_scales, b1, gamma1, be
 
         FIRST_TAPS = (0, 1, 3, 2, 4)
         LATER_TAPS = (0, 1, 2, 4, 3)
+        AHEAD = 4
 
-        load_x(0)
-        load_x(PAIRS - 1)
-        for r in range(4):
-            nc.sync.dma_start(out=w_scales_first[r:P:32, :, :].bitcast(I32), in_=s_view[r][:, 0 : TAPS * L : L, :].bitcast(I32))
-        load_w(0, FIRST_TAPS)
-        load_x(1)
-        load_w(1, LATER_TAPS)
-        load_x(2)
-        for l in range(2, L):
+        load_x(0, 0)
+        load_x(0, 1)
+        load_scales(0)
+        load_w(0, (0,))
+        load_x(PAIRS - 1, 0)
+        load_w(0, (1,))
+        load_x(PAIRS - 1, 1)
+        load_w(0, (3, 2, 4))
+        for l in range(1, AHEAD):
+            if l < PAIRS - 1:
+                load_x(l, 0)
+                load_x(l, 1)
+            load_scales(l)
             load_w(l, LATER_TAPS)
 
         def transpose_chunk(m, pair, copy):
             xt = psum_xt.tile([P, 2, 2, P], F32, tag="xt")
             for li in range(2):
-                words = x_sb[:, m, 2 * pair + li, :].bitcast(F32)
+                words = x_sb[:, pair, m, li, :].bitcast(F32)
                 for u in range(2):
                     nc.tensor.transpose(xt[:, li, u, :], words[:, u : C // 2 : 2], ident[:])
             grouped = stage.tile([P, 2, P, PACK], BF16, align_bytes=64)
@@ -161,21 +169,8 @@ def tile_residualblock5_pa_t_e_kernel(tc, x, k1_words, k1_scales, b1, gamma1, be
             quantise_chunk(*waiting[quantised[0]])
             quantised[0] += 1
 
-        nc.vector.tensor_copy(out=raw[:], in_=raw_bf[:])
-        head = [(m, pair) for pair in (0, PAIRS - 1) for m in range(B_TILES)]
-        for n, (m, pair) in enumerate(head):
-            waiting.append(transpose_chunk(m, pair, nc.scalar.copy if n % 2 == 0 else nc.vector.tensor_copy))
-            if n >= 1:
-                quantise_next()
-            if n == 1:
-                vectors_to_columns()
-            if n == 2:
-                nc.scalar.sqrt(out=std[:], in_=var_eps[:])
-            if n == 3:
-                gain_and_shift()
-            if n == 5:
-                nc.scalar.copy(out=gain_bc[:], in_=spread_row(GAIN))
-        quantise_next()
+        def chunk(m, pair, copy):
+            waiting.append(transpose_chunk(m, pair, copy))
 
         def product(bank, l, m, i, taps):
             src = (l - TAP_STEP[i]) % L
@@ -184,7 +179,7 @@ def tile_residualblock5_pa_t_e_kernel(tc, x, k1_words, k1_scales, b1, gamma1, be
                 lhsT=x_codes[:, m, src, :].bitcast(FP8X4),
                 lhsT_scale=x_scales[:, m, src, :],
                 rhs=w_codes[:, l, i, :].bitcast(FP8X4),
-                rhs_scale=w_scales_first[:, i, :] if l == 0 else w_scales[:, L * i + l, :],
+                rhs_scale=w_scales[l][:, i, :],
                 start=(i == taps[0]),
                 stop=(i == taps[-1]),
             )
@@ -195,6 +190,9 @@ def tile_residualblock5_pa_t_e_kernel(tc, x, k1_words, k1_scales, b1, gamma1, be
             nc.scalar.activation(out=lift[:], in_=z[:], func=ACT.Relu, scale=LEAKY_ALPHA - 1.0)
             nc.gpsimd.tensor_tensor(out=z[:], in0=z[:], in1=lift[:], op=ALU.add)
             nc.sync.dma_start(out=out_view[:, m, l, :], in_=z[:])
+            if m == B_TILES - 1 and l + AHEAD < L:
+                load_scales(l + AHEAD)
+                load_w(l + AHEAD, LATER_TAPS)
 
         emptied = []
 
@@ -205,35 +203,63 @@ def tile_residualblock5_pa_t_e_kernel(tc, x, k1_words, k1_scales, b1, gamma1, be
                 finish(*emptied[-1])
             emptied.append((l, m, z, shift_ps))
 
-        def prepare(l):
-            if l in (1, 2):
-                for m in range(B_TILES):
-                    waiting.append(transpose_chunk(m, l, nc.scalar.copy))
-            return spread_row(l)
+        def taps_over_banks(banks, l, first_m, taps, all_taps):
+            for i in taps:
+                for k in range(len(banks)):
+                    product(banks[k], l, first_m + k, i, all_taps)
 
-        shift_ps = prepare(0)
+        LAST = PAIRS - 1
         banks = [psum_acc.tile([P, F], F32, name="acc") for m in range(B_TILES)]
-        for i in FIRST_TAPS:
-            for m in range(B_TILES):
-                product(banks[m], 0, m, i, FIRST_TAPS)
-        next_shift = prepare(1)
+        nc.vector.tensor_copy(out=raw[:], in_=raw_bf[:])
+        chunk(0, 0, nc.scalar.copy)
+        chunk(1, 0, nc.vector.tensor_copy)
+        quantise_next()
+        vectors_to_columns()
+        chunk(2, 0, nc.scalar.copy)
+        quantise_next()
+        nc.scalar.sqrt(out=std[:], in_=var_eps[:])
+        chunk(3, 0, nc.vector.tensor_copy)
+        quantise_next()
+        gain_and_shift()
+        quantise_next()
+        taps_over_banks(banks, 0, 0, (0,), FIRST_TAPS)
+        chunk(0, LAST, nc.scalar.copy)
+        chunk(1, LAST, nc.vector.tensor_copy)
+        quantise_next()
+        nc.scalar.copy(out=gain_bc[:], in_=spread_row(GAIN))
+        quantise_next()
+        taps_over_banks(banks, 0, 0, (1,), FIRST_TAPS)
+        chunk(2, LAST, nc.scalar.copy)
+        chunk(3, LAST, nc.vector.tensor_copy)
+        quantise_next()
+        shift_ps = spread_row(0)
+        quantise_next()
+        taps_over_banks(banks, 0, 0, (3, 2, 4), FIRST_TAPS)
+
+        def between(l, pair):
+            newer = l + 1 if pair == 1 else l
+            if 1 <= newer < LAST:
+                first_m = 0 if pair == 1 else 2
+                chunk(first_m, newer, nc.scalar.copy)
+                chunk(first_m + 1, newer, nc.scalar.copy)
+            if pair == 1 and l + 1 < L:
+                return spread_row(l + 1)
+            return None
+
+        next_shift = between(0, 1)
         for m in range(B_TILES):
             empty(banks[m], 0, m, shift_ps)
-            if m >= 1:
+            if m >= 1 and quantised[0] < len(waiting):
                 quantise_next()
-        quantise_next()
 
         for l in range(1, L):
             shift_ps = next_shift
             for pair in range(B_TILES // 2):
                 banks = [psum_acc.tile([P, F], F32, name="acc") for k in range(2)]
-                for i in LATER_TAPS:
-                    for k in range(2):
-                        product(banks[k], l, 2 * pair + k, i, LATER_TAPS)
+                taps_over_banks(banks, l, 2 * pair, LATER_TAPS, LATER_TAPS)
+                next_shift = between(l, pair)
                 for k in range(2):
                     empty(banks[k], l, 2 * pair + k, shift_ps)
                     if quantised[0] < len(waiting):
                         quantise_next()
-            if l + 1 < L:
-                next_shift = prepare(l + 1)
         finish(*emptied[-1])

@@ -172,36 +172,47 @@ def tile_residualblock5_pa_t_e_kernel(tc, x, k1_words, k1_scales, b1, gamma1, be
         def chunk(m, pair, copy):
             waiting.append(transpose_chunk(m, pair, copy))
 
-        def product(bank, l, m, i, taps):
+        ALL = slice(0, F)
+
+        def product(bank, l, m, i, taps, cols=ALL):
             src = (l - TAP_STEP[i]) % L
             nc.tensor.matmul_mx(
                 out=bank[:],
                 lhsT=x_codes[:, m, src, :].bitcast(FP8X4),
                 lhsT_scale=x_scales[:, m, src, :],
-                rhs=w_codes[:, l, i, :].bitcast(FP8X4),
-                rhs_scale=w_scales[l][:, i, :],
+                rhs=w_codes[:, l, i, cols].bitcast(FP8X4),
+                rhs_scale=w_scales[l][:, i, cols],
                 start=(i == taps[0]),
                 stop=(i == taps[-1]),
             )
 
-        def finish(l, m, z, shift_ps):
-            nc.vector.tensor_tensor(out=z[:], in0=z[:], in1=shift_ps, op=ALU.add)
-            lift = scratch.tile([P, F], F32)
+        def add_shift(l, m, z, shift_ps, cols):
+            nc.vector.tensor_tensor(out=z[:], in0=z[:], in1=shift_ps[:, cols], op=ALU.add)
+
+        def bend_on_scalar_and_gpsimd(l, m, z, shift_ps, cols):
+            lift = scratch.tile([P, F], F32, tag="lift")
             nc.scalar.activation(out=lift[:], in_=z[:], func=ACT.Relu, scale=LEAKY_ALPHA - 1.0)
             nc.gpsimd.tensor_tensor(out=z[:], in0=z[:], in1=lift[:], op=ALU.add)
-            nc.sync.dma_start(out=out_view[:, m, l, :], in_=z[:])
+            nc.sync.dma_start(out=out_view[:, m, l, cols], in_=z[:])
             if m == B_TILES - 1 and l + AHEAD < L:
                 load_scales(l + AHEAD)
                 load_w(l + AHEAD, LATER_TAPS)
 
+        def bend_on_vector(l, m, z, shift_ps, cols):
+            bent = scratch.tile([P, cols.stop - cols.start], F32, tag="lift")
+            nc.vector.scalar_tensor_tensor(out=bent[:], in0=z[:], scalar=LEAKY_ALPHA, in1=z[:], op0=ALU.mult, op1=ALU.max)
+            nc.sync.dma_start(out=out_view[:, m, l, cols], in_=bent[:])
+
         emptied = []
 
-        def empty(bank, l, m, shift_ps):
-            z = results.tile([P, F], F32)
-            nc.vector.tensor_tensor(out=z[:], in0=bank[:], in1=gain_bc[:], op=ALU.mult)
+        def empty(bank, l, m, shift_ps, cols=ALL, bend_last=True):
+            z = results.tile([P, cols.stop - cols.start], F32, tag="z")
+            nc.vector.tensor_tensor(out=z[:], in0=bank[:], in1=gain_bc[:, cols], op=ALU.mult)
             if emptied:
-                finish(*emptied[-1])
-            emptied.append((l, m, z, shift_ps))
+                add_shift(*emptied[-1])
+                if bend_last:
+                    bend_on_scalar_and_gpsimd(*emptied[-1])
+            emptied.append((l, m, z, shift_ps, cols))
 
         def taps_over_banks(banks, l, first_m, taps, all_taps):
             for i in taps:
@@ -214,24 +225,24 @@ def tile_residualblock5_pa_t_e_kernel(tc, x, k1_words, k1_scales, b1, gamma1, be
         chunk(0, 0, nc.scalar.copy)
         chunk(1, 0, nc.vector.tensor_copy)
         quantise_next()
-        vectors_to_columns()
         chunk(2, 0, nc.scalar.copy)
         quantise_next()
-        nc.scalar.sqrt(out=std[:], in_=var_eps[:])
         chunk(3, 0, nc.vector.tensor_copy)
         quantise_next()
-        gain_and_shift()
         quantise_next()
+        vectors_to_columns()
+        nc.scalar.sqrt(out=std[:], in_=var_eps[:])
         taps_over_banks(banks, 0, 0, (0,), FIRST_TAPS)
         chunk(0, LAST, nc.scalar.copy)
         chunk(1, LAST, nc.vector.tensor_copy)
         quantise_next()
-        nc.scalar.copy(out=gain_bc[:], in_=spread_row(GAIN))
+        gain_and_shift()
         quantise_next()
         taps_over_banks(banks, 0, 0, (1,), FIRST_TAPS)
         chunk(2, LAST, nc.scalar.copy)
         chunk(3, LAST, nc.vector.tensor_copy)
         quantise_next()
+        nc.scalar.copy(out=gain_bc[:], in_=spread_row(GAIN))
         shift_ps = spread_row(0)
         quantise_next()
         taps_over_banks(banks, 0, 0, (3, 2, 4), FIRST_TAPS)
@@ -252,7 +263,7 @@ def tile_residualblock5_pa_t_e_kernel(tc, x, k1_words, k1_scales, b1, gamma1, be
             if m >= 1 and quantised[0] < len(waiting):
                 quantise_next()
 
-        for l in range(1, L):
+        for l in range(1, L - 1):
             shift_ps = next_shift
             for pair in range(B_TILES // 2):
                 banks = [psum_acc.tile([P, F], F32, name="acc") for k in range(2)]
@@ -262,4 +273,17 @@ def tile_residualblock5_pa_t_e_kernel(tc, x, k1_words, k1_scales, b1, gamma1, be
                     empty(banks[k], l, 2 * pair + k, shift_ps)
                     if quantised[0] < len(waiting):
                         quantise_next()
-        finish(*emptied[-1])
+
+        l = L - 1
+        shift_ps = next_shift
+        HALVES = (slice(0, F // 2), slice(F // 2, F))
+        pieces = [(m, ALL) for m in range(B_TILES - 1)] + [(B_TILES - 1, cols) for cols in HALVES]
+        OWN = 3
+        for n, (m, cols) in enumerate(pieces):
+            bank = psum_acc.tile([P, cols.stop - cols.start], F32, name="acc")
+            for i in LATER_TAPS:
+                product(bank, l, m, i, LATER_TAPS, cols)
+            empty(bank, l, m, shift_ps, cols, bend_last=(n <= len(pieces) - OWN))
+        add_shift(*emptied[-1])
+        for piece in emptied[-OWN:]:
+            bend_on_vector(*piece)

@@ -36,6 +36,7 @@ def tile_residualblock5_pa_t_e_kernel(tc, x, k1_words, k1_scales, b1, gamma1, be
         ctx.enter_context(tc.manual_schedule())
         keep = ctx.enter_context(tc.tile_pool(name="keep", bufs=1))
         stage = ctx.enter_context(tc.tile_pool(name="stage", bufs=4))
+        sorting = ctx.enter_context(tc.tile_pool(name="sorting", bufs=4))
         results = ctx.enter_context(tc.tile_pool(name="results", bufs=16))
         scratch = ctx.enter_context(tc.tile_pool(name="scratch", bufs=3))
         psum_xt = ctx.enter_context(tc.psum_pool(name="psum_xt", bufs=2))
@@ -108,12 +109,25 @@ def tile_residualblock5_pa_t_e_kernel(tc, x, k1_words, k1_scales, b1, gamma1, be
             load_scales(l)
             load_w(l, LATER_TAPS)
 
+        sorted_words = {}
+
+        def sort_words(m, pair):
+            by_parity = sorting.tile([P, 2, 2, P], F32)
+            nc.scalar.copy(
+                out=by_parity[:],
+                in_=x_sb[:, pair, m, :, :].bitcast(F32).rearrange("p l (j u) -> p l u j", u=2),
+            )
+            sorted_words[(m, pair)] = by_parity
+
         def transpose_chunk(m, pair, copy):
             xt = psum_xt.tile([P, 2, 2, P], F32, tag="xt")
             for li in range(2):
                 words = x_sb[:, pair, m, li, :].bitcast(F32)
                 for u in range(2):
-                    nc.tensor.transpose(xt[:, li, u, :], words[:, u : C // 2 : 2], ident[:])
+                    if (m, pair) in sorted_words:
+                        nc.tensor.transpose(xt[:, li, u, :], sorted_words[(m, pair)][:, li, u, :], ident[:])
+                    else:
+                        nc.tensor.transpose(xt[:, li, u, :], words[:, u : C // 2 : 2], ident[:])
             grouped = stage.tile([P, 2, P, PACK], BF16, align_bytes=64)
             copy(out=grouped[:].bitcast(F32), in_=xt[:].rearrange("p l u b -> p l b u"))
             return (m, pair, grouped)
@@ -230,9 +244,13 @@ def tile_residualblock5_pa_t_e_kernel(tc, x, k1_words, k1_scales, b1, gamma1, be
         chunk(3, 0, nc.vector.tensor_copy)
         quantise_next()
         quantise_next()
+        sort_words(0, LAST)
+        sort_words(1, LAST)
         vectors_to_columns()
         nc.scalar.sqrt(out=std[:], in_=var_eps[:])
         taps_over_banks(banks, 0, 0, (0,), FIRST_TAPS)
+        sort_words(2, LAST)
+        sort_words(3, LAST)
         chunk(0, LAST, nc.scalar.copy)
         chunk(1, LAST, nc.vector.tensor_copy)
         quantise_next()
@@ -245,6 +263,8 @@ def tile_residualblock5_pa_t_e_kernel(tc, x, k1_words, k1_scales, b1, gamma1, be
         nc.scalar.copy(out=gain_bc[:], in_=spread_row(GAIN))
         shift_ps = spread_row(0)
         quantise_next()
+        sort_words(0, 1)
+        sort_words(1, 1)
         taps_over_banks(banks, 0, 0, (3, 2, 4), FIRST_TAPS)
 
         def between(l, pair):
@@ -253,6 +273,10 @@ def tile_residualblock5_pa_t_e_kernel(tc, x, k1_words, k1_scales, b1, gamma1, be
                 first_m = 0 if pair == 1 else 2
                 chunk(first_m, newer, nc.scalar.copy)
                 chunk(first_m + 1, newer, nc.scalar.copy)
+                after = (2, newer) if pair == 1 else (0, newer + 1)
+                if after[1] < LAST:
+                    sort_words(after[0], after[1])
+                    sort_words(after[0] + 1, after[1])
             if pair == 1 and l + 1 < L:
                 return spread_row(l + 1)
             return None

@@ -37,7 +37,7 @@ def tile_residualblock5_pa_t_e_kernel(tc, x, k1_words, k1_scales, b1, gamma1, be
         keep = ctx.enter_context(tc.tile_pool(name="keep", bufs=1))
         stage = ctx.enter_context(tc.tile_pool(name="stage", bufs=4))
         sorting = ctx.enter_context(tc.tile_pool(name="sorting", bufs=4))
-        results = ctx.enter_context(tc.tile_pool(name="results", bufs=16))
+        results = ctx.enter_context(tc.tile_pool(name="results", bufs=8))
         scratch = ctx.enter_context(tc.tile_pool(name="scratch", bufs=3))
         psum_xt = ctx.enter_context(tc.psum_pool(name="psum_xt", bufs=2))
         psum_row = ctx.enter_context(tc.psum_pool(name="psum_row", bufs=2))
@@ -86,9 +86,10 @@ def tile_residualblock5_pa_t_e_kernel(tc, x, k1_words, k1_scales, b1, gamma1, be
                     out=w_scales[l][r:P:32, :, :].bitcast(I32), in_=s_view[r][:, l : TAPS * L : L, :].bitcast(I32)
                 )
 
-        def load_w(l, taps):
-            for i in taps:
-                nc.sync.dma_start(out=w_codes[:, l, i, :].bitcast(I32), in_=w_view[l][:, i, :].bitcast(I32))
+        def load_w(l, first, stop):
+            nc.sync.dma_start(
+                out=w_codes[:, l, first:stop, :].bitcast(I32), in_=w_view[l][:, first:stop, :].bitcast(I32)
+            )
 
         FIRST_TAPS = (0, 1, 3, 2, 4)
         LATER_TAPS = (0, 1, 2, 4, 3)
@@ -97,17 +98,21 @@ def tile_residualblock5_pa_t_e_kernel(tc, x, k1_words, k1_scales, b1, gamma1, be
         load_x(0, 0)
         load_x(0, 1)
         load_scales(0)
-        load_w(0, (0,))
+        load_w(0, 0, 1)
         load_x(PAIRS - 1, 0)
-        load_w(0, (1,))
+        load_w(0, 1, 2)
         load_x(PAIRS - 1, 1)
-        load_w(0, (3, 2, 4))
+        load_w(0, 2, TAPS)
         for l in range(1, AHEAD):
             if l < PAIRS - 1:
                 load_x(l, 0)
                 load_x(l, 1)
             load_scales(l)
-            load_w(l, LATER_TAPS)
+            if l == 1:
+                load_w(l, 0, 2)
+                load_w(l, 2, TAPS)
+            else:
+                load_w(l, 0, TAPS)
 
         sorted_words = {}
 
@@ -201,27 +206,38 @@ def tile_residualblock5_pa_t_e_kernel(tc, x, k1_words, k1_scales, b1, gamma1, be
             )
 
         def add_shift(l, m, z, shift_ps, cols):
-            nc.vector.tensor_tensor(out=z[:], in0=z[:], in1=shift_ps[:, cols], op=ALU.add)
+            nc.vector.tensor_tensor(out=z, in0=z, in1=shift_ps[:, cols], op=ALU.add)
 
         def bend_on_scalar_and_gpsimd(l, m, z, shift_ps, cols):
             lift = scratch.tile([P, F], F32, tag="lift")
-            nc.scalar.activation(out=lift[:], in_=z[:], func=ACT.Relu, scale=LEAKY_ALPHA - 1.0)
-            nc.gpsimd.tensor_tensor(out=z[:], in0=z[:], in1=lift[:], op=ALU.add)
-            nc.sync.dma_start(out=out_view[:, m, l, cols], in_=z[:])
+            nc.scalar.activation(out=lift[:], in_=z, func=ACT.Relu, scale=LEAKY_ALPHA - 1.0)
+            nc.gpsimd.tensor_tensor(out=z, in0=z, in1=lift[:], op=ALU.add)
+            if l == L - 1:
+                nc.sync.dma_start(out=out_view[:, m, l, cols], in_=z)
+            elif m % 2 == 1:
+                nc.sync.dma_start(out=out_view[:, m - 1 : m + 1, l, :], in_=doubles[(l, m // 2)][:])
             if m == B_TILES - 1 and l + AHEAD < L:
                 load_scales(l + AHEAD)
-                load_w(l + AHEAD, LATER_TAPS)
+                load_w(l + AHEAD, 0, TAPS)
 
         def bend_on_vector(l, m, z, shift_ps, cols):
             bent = scratch.tile([P, cols.stop - cols.start], F32, tag="lift")
-            nc.vector.scalar_tensor_tensor(out=bent[:], in0=z[:], scalar=LEAKY_ALPHA, in1=z[:], op0=ALU.mult, op1=ALU.max)
+            nc.vector.scalar_tensor_tensor(out=bent[:], in0=z, scalar=LEAKY_ALPHA, in1=z, op0=ALU.mult, op1=ALU.max)
             nc.sync.dma_start(out=out_view[:, m, l, cols], in_=bent[:])
 
         emptied = []
+        doubles = {}
 
         def empty(bank, l, m, shift_ps, cols=ALL, bend_last=True):
-            z = results.tile([P, cols.stop - cols.start], F32, tag="z")
-            nc.vector.tensor_tensor(out=z[:], in0=bank[:], in1=gain_bc[:, cols], op=ALU.mult)
+            if l == L - 1:
+                single = results.tile([P, cols.stop - cols.start], F32, tag="z")
+                z = single[:]
+            else:
+                if m % 2 == 0:
+                    double = results.tile([P, 2, F], F32, tag="z")
+                    doubles[(l, m // 2)] = double
+                z = doubles[(l, m // 2)][:, m % 2, :]
+            nc.vector.tensor_tensor(out=z, in0=bank[:], in1=gain_bc[:, cols], op=ALU.mult)
             if emptied:
                 add_shift(*emptied[-1])
                 if bend_last:

@@ -49,7 +49,7 @@ def tile_residualblock5_pa_t_e_kernel(tc, x, k1_words, k1_scales, b1, gamma1, be
         w_codes = keep.tile([P, L, TAPS, F], U32, align_bytes=64)
         w_scales = [keep.tile([P, TAPS, F], U8, align_bytes=64, name="w_scales_%d" % l) for l in range(L)]
         ident = keep.tile([P, P], F32)
-        raw_bf = keep.tile([P, F], BF16)
+        raw_bf = keep.tile([ROW_VAR + 1, F], BF16)
         raw = keep.tile([P, F], F32)
         cols = keep.tile([P, F_TILES, ROWS], F32)
         var_eps = keep.tile([P, F_TILES], F32)
@@ -58,15 +58,15 @@ def tile_residualblock5_pa_t_e_kernel(tc, x, k1_words, k1_scales, b1, gamma1, be
         spread = keep.tile([P, F_TILES, L + 1], F32)
         gain_bc = keep.tile([P, F], F32)
 
-        nc.vector.memset(raw_bf[:], 0.0)
+        nc.vector.memset(raw[:], 0.0)
         nc.vector.memset(var_eps[:], 1.0)
         for l in range(L):
             nc.vector.memset(w_scales[l][:].rearrange("p i n -> p (i n)").bitcast(I32), 0)
         make_identity(nc, ident[:])
 
-        nc.scalar.dma_start(out=raw_bf[0:L, :], in_=b1)
+        nc.sync.dma_start(out=raw_bf[0:L, :], in_=b1)
         for row, vec in ((ROW_GAMMA, gamma1), (ROW_BETA, beta1), (ROW_MEAN, mean1), (ROW_VAR, var1)):
-            nc.scalar.dma_start(out=raw_bf[row : row + 1, :], in_=vec.unsqueeze(0))
+            nc.sync.dma_start(out=raw_bf[row : row + 1, :], in_=vec.unsqueeze(0))
         nc.scalar.sqrt(out=std[:], in_=var_eps[:])
 
         x_view = x.rearrange("(m p) l c -> p m l c", p=P)
@@ -103,16 +103,17 @@ def tile_residualblock5_pa_t_e_kernel(tc, x, k1_words, k1_scales, b1, gamma1, be
         load_w(0, 1, 2)
         load_x(PAIRS - 1, 1)
         load_w(0, 2, TAPS)
-        for l in range(1, AHEAD):
-            if l < PAIRS - 1:
-                load_x(l, 0)
-                load_x(l, 1)
-            load_scales(l)
-            if l == 1:
-                load_w(l, 0, 2)
-                load_w(l, 2, TAPS)
-            else:
-                load_w(l, 0, TAPS)
+        load_x(1, 0)
+        load_scales(1)
+        load_w(1, 0, 2)
+        load_w(1, 2, TAPS)
+        load_x(1, 1)
+        load_scales(2)
+        load_w(2, 0, TAPS)
+        load_x(2, 0)
+        load_x(2, 1)
+        load_scales(3)
+        load_w(3, 0, TAPS)
 
         sorted_words = {}
 
@@ -251,7 +252,7 @@ def tile_residualblock5_pa_t_e_kernel(tc, x, k1_words, k1_scales, b1, gamma1, be
 
         LAST = PAIRS - 1
         banks = [psum_acc.tile([P, F], F32, name="acc") for m in range(B_TILES)]
-        nc.vector.tensor_copy(out=raw[:], in_=raw_bf[:])
+        nc.vector.tensor_copy(out=raw[0 : ROW_VAR + 1, :], in_=raw_bf[:])
         chunk(0, 0, nc.scalar.copy)
         chunk(1, 0, nc.vector.tensor_copy)
         quantise_next()

@@ -60,9 +60,12 @@ def tile_residualblock5_pa_t_e_kernel(tc, x, k1_words, k1_scales, b1, gamma1, be
 
         nc.vector.memset(raw[:], 0.0)
         nc.vector.memset(var_eps[:], 1.0)
-        for l in range(L):
+        ON_VECTOR = 2
+        for l in range(ON_VECTOR):
             nc.vector.memset(w_scales[l][:].rearrange("p i n -> p (i n)").bitcast(I32), 0)
         make_identity(nc, ident[:])
+        for l in range(ON_VECTOR, L):
+            nc.gpsimd.memset(w_scales[l][:].rearrange("p i n -> p (i n)").bitcast(F32), 0.0)
 
         nc.sync.dma_start(out=raw_bf[0:L, :], in_=b1)
         for row, vec in ((ROW_GAMMA, gamma1), (ROW_BETA, beta1), (ROW_MEAN, mean1), (ROW_VAR, var1)):
@@ -206,44 +209,61 @@ def tile_residualblock5_pa_t_e_kernel(tc, x, k1_words, k1_scales, b1, gamma1, be
                 stop=(i == taps[-1]),
             )
 
-        def add_shift(l, m, z, shift_ps, cols):
+        HALVES = (slice(0, F // 2), slice(F // 2, F))
+
+        def times_gain(bank, z, cols):
+            nc.vector.tensor_tensor(out=z, in0=bank, in1=gain_bc[:, cols], op=ALU.mult)
+
+        def add_shift(z, shift_ps, cols):
             nc.vector.tensor_tensor(out=z, in0=z, in1=shift_ps[:, cols], op=ALU.add)
 
-        def bend_on_scalar_and_gpsimd(l, m, z, shift_ps, cols):
+        def bend_on_scalar_and_gpsimd(z):
             lift = scratch.tile([P, F], F32, tag="lift")
             nc.scalar.activation(out=lift[:], in_=z, func=ACT.Relu, scale=LEAKY_ALPHA - 1.0)
             nc.gpsimd.tensor_tensor(out=z, in0=z, in1=lift[:], op=ALU.add)
-            if l == L - 1:
-                nc.sync.dma_start(out=out_view[:, m, l, cols], in_=z)
-            elif m % 2 == 1:
+
+        def bend_on_vector(z):
+            nc.vector.scalar_tensor_tensor(out=z, in0=z, scalar=LEAKY_ALPHA, in1=z, op0=ALU.mult, op1=ALU.max)
+
+        doubles = {}
+
+        def result_of(l, m):
+            if m % 2 == 0:
+                double = results.tile([P, 2, F], F32, tag="z")
+                doubles[(l, m // 2)] = double
+            return doubles[(l, m // 2)][:, m % 2, :]
+
+        def store_double(l, m):
+            if m % 2 == 1:
                 nc.sync.dma_start(out=out_view[:, m - 1 : m + 1, l, :], in_=doubles[(l, m // 2)][:])
             if m == B_TILES - 1 and l + AHEAD < L:
                 load_scales(l + AHEAD)
                 load_w(l + AHEAD, 0, TAPS)
 
-        def bend_on_vector(l, m, z, shift_ps, cols):
-            bent = scratch.tile([P, cols.stop - cols.start], F32, tag="lift")
-            nc.vector.scalar_tensor_tensor(out=bent[:], in0=z, scalar=LEAKY_ALPHA, in1=z, op0=ALU.mult, op1=ALU.max)
-            nc.sync.dma_start(out=out_view[:, m, l, cols], in_=bent[:])
+        def quantise_if_any():
+            if quantised[0] < len(waiting):
+                quantise_next()
 
-        emptied = []
-        doubles = {}
+        def finish(l, m, z, shift_ps):
+            add_shift(z, shift_ps, ALL)
+            bend_on_scalar_and_gpsimd(z)
+            store_double(l, m)
 
-        def empty(bank, l, m, shift_ps, cols=ALL, bend_last=True):
-            if l == L - 1:
-                single = results.tile([P, cols.stop - cols.start], F32, tag="z")
-                z = single[:]
-            else:
-                if m % 2 == 0:
-                    double = results.tile([P, 2, F], F32, tag="z")
-                    doubles[(l, m // 2)] = double
-                z = doubles[(l, m // 2)][:, m % 2, :]
-            nc.vector.tensor_tensor(out=z, in0=bank[:], in1=gain_bc[:, cols], op=ALU.mult)
-            if emptied:
-                add_shift(*emptied[-1])
-                if bend_last:
-                    bend_on_scalar_and_gpsimd(*emptied[-1])
-            emptied.append((l, m, z, shift_ps, cols))
+        def empty_pair(banks, l, first_m, shift_ps):
+            pair_z = []
+            for k in range(2):
+                pair_z.append(result_of(l, first_m + k))
+                times_gain(banks[k][:], pair_z[k], ALL)
+            for k in range(2):
+                quantise_if_any()
+                finish(l, first_m + k, pair_z[k], shift_ps)
+
+        def empty_alone(bank, z, shift_ps):
+            for cols in HALVES:
+                times_gain(bank[:, cols], z[:, cols], cols)
+            for cols in HALVES:
+                add_shift(z[:, cols], shift_ps, cols)
+            bend_on_scalar_and_gpsimd(z)
 
         def taps_over_banks(banks, l, first_m, taps, all_taps):
             for i in taps:
@@ -282,7 +302,8 @@ def tile_residualblock5_pa_t_e_kernel(tc, x, k1_words, k1_scales, b1, gamma1, be
         quantise_next()
         sort_words(0, 1)
         sort_words(1, 1)
-        taps_over_banks(banks, 0, 0, (3, 2, 4), FIRST_TAPS)
+        for m in range(B_TILES):
+            taps_over_banks(banks[m : m + 1], 0, m, (3, 2, 4), FIRST_TAPS)
 
         def between(l, pair):
             newer = l + 1 if pair == 1 else l
@@ -298,33 +319,57 @@ def tile_residualblock5_pa_t_e_kernel(tc, x, k1_words, k1_scales, b1, gamma1, be
                 return spread_row(l + 1)
             return None
 
-        next_shift = between(0, 1)
+        zs = []
         for m in range(B_TILES):
-            empty(banks[m], 0, m, shift_ps)
-            if m >= 1 and quantised[0] < len(waiting):
-                quantise_next()
+            if m == B_TILES - 1:
+                next_shift = between(0, 1)
+            zs.append(result_of(0, m))
+            times_gain(banks[m][:], zs[m], ALL)
+            if m == B_TILES - 1:
+                quantise_if_any()
+            if m >= 1:
+                finish(0, m - 1, zs[m - 1], shift_ps)
+        quantise_if_any()
+        finish(0, B_TILES - 1, zs[B_TILES - 1], shift_ps)
 
-        for l in range(1, L - 1):
+        ALONE = 2
+        for l in range(1, L - ALONE):
             shift_ps = next_shift
             for pair in range(B_TILES // 2):
                 banks = [psum_acc.tile([P, F], F32, name="acc") for k in range(2)]
                 taps_over_banks(banks, l, 2 * pair, LATER_TAPS, LATER_TAPS)
                 next_shift = between(l, pair)
-                for k in range(2):
-                    empty(banks[k], l, 2 * pair + k, shift_ps)
-                    if quantised[0] < len(waiting):
-                        quantise_next()
+                empty_pair(banks, l, 2 * pair, shift_ps)
 
-        l = L - 1
-        shift_ps = next_shift
-        HALVES = (slice(0, F // 2), slice(F // 2, F))
-        pieces = [(m, ALL) for m in range(B_TILES - 1)] + [(B_TILES - 1, cols) for cols in HALVES]
-        OWN = 3
-        for n, (m, cols) in enumerate(pieces):
+        def fill(l, m, cols):
             bank = psum_acc.tile([P, cols.stop - cols.start], F32, name="acc")
             for i in LATER_TAPS:
                 product(bank, l, m, i, LATER_TAPS, cols)
-            empty(bank, l, m, shift_ps, cols, bend_last=(n <= len(pieces) - OWN))
-        add_shift(*emptied[-1])
-        for piece in emptied[-OWN:]:
-            bend_on_vector(*piece)
+            return bank
+
+        l = L - 2
+        shift_ps = next_shift
+        for m in range(B_TILES):
+            bank = fill(l, m, ALL)
+            if m == B_TILES - 1:
+                next_shift = spread_row(L - 1)
+            empty_alone(bank, result_of(l, m), shift_ps)
+            store_double(l, m)
+
+        l = L - 1
+        shift_ps = next_shift
+        for m in range(B_TILES - 1):
+            bank = fill(l, m, ALL)
+            single = results.tile([P, F], F32, tag="z")
+            empty_alone(bank, single[:], shift_ps)
+            nc.sync.dma_start(out=out_view[:, m, l, :], in_=single[:])
+        m = B_TILES - 1
+        single = results.tile([P, F], F32, tag="z")
+        for cols in HALVES:
+            bank = fill(l, m, cols)
+            times_gain(bank[:], single[:, cols], cols)
+        for cols in HALVES:
+            add_shift(single[:, cols], shift_ps, cols)
+        for cols in HALVES:
+            bend_on_vector(single[:, cols])
+            nc.sync.dma_start(out=out_view[:, m, l, cols], in_=single[:, cols])

@@ -60,12 +60,13 @@ def tile_residualblock5_pa_t_e_kernel(tc, x, k1_words, k1_scales, b1, gamma1, be
 
         nc.vector.memset(raw[:], 0.0)
         nc.vector.memset(var_eps[:], 1.0)
-        ON_VECTOR = 2
-        for l in range(ON_VECTOR):
+        def zero_planes(l):
             nc.vector.memset(w_scales[l][:].rearrange("p i n -> p (i n)").bitcast(I32), 0)
+
+        ZEROED_FIRST = 6
+        for l in range(ZEROED_FIRST):
+            zero_planes(l)
         make_identity(nc, ident[:])
-        for l in range(ON_VECTOR, L):
-            nc.gpsimd.memset(w_scales[l][:].rearrange("p i n -> p (i n)").bitcast(F32), 0.0)
 
         nc.sync.dma_start(out=raw_bf[0:L, :], in_=b1)
         for row, vec in ((ROW_GAMMA, gamma1), (ROW_BETA, beta1), (ROW_MEAN, mean1), (ROW_VAR, var1)):
@@ -285,6 +286,8 @@ def tile_residualblock5_pa_t_e_kernel(tc, x, k1_words, k1_scales, b1, gamma1, be
         sort_words(1, LAST)
         vectors_to_columns()
         nc.scalar.sqrt(out=std[:], in_=var_eps[:])
+        for l in range(ZEROED_FIRST, L):
+            zero_planes(l)
         taps_over_banks(banks, 0, 0, (0,), FIRST_TAPS)
         sort_words(2, LAST)
         sort_words(3, LAST)

@@ -255,16 +255,9 @@ def tile_residualblock5_pa_t_e_kernel(tc, x, k1_words, k1_scales, b1, gamma1, be
             for k in range(2):
                 pair_z.append(result_of(l, first_m + k))
                 times_gain(banks[k][:], pair_z[k], ALL)
+                catch_up()
             for k in range(2):
-                quantise_if_any()
                 finish(l, first_m + k, pair_z[k], shift_ps)
-
-        def empty_alone(bank, z, shift_ps):
-            for cols in HALVES:
-                times_gain(bank[:, cols], z[:, cols], cols)
-            for cols in HALVES:
-                add_shift(z[:, cols], shift_ps, cols)
-            bend_on_scalar_and_gpsimd(z)
 
         def taps_over_banks(banks, l, first_m, taps, all_taps):
             for i in taps:
@@ -305,8 +298,7 @@ def tile_residualblock5_pa_t_e_kernel(tc, x, k1_words, k1_scales, b1, gamma1, be
         quantise_next()
         sort_words(0, 1)
         sort_words(1, 1)
-        for m in range(B_TILES):
-            taps_over_banks(banks[m : m + 1], 0, m, (3, 2, 4), FIRST_TAPS)
+        taps_over_banks(banks, 0, 0, (3, 2, 4), FIRST_TAPS)
 
         def between(l, pair):
             newer = l + 1 if pair == 1 else l
@@ -322,19 +314,25 @@ def tile_residualblock5_pa_t_e_kernel(tc, x, k1_words, k1_scales, b1, gamma1, be
                 return spread_row(l + 1)
             return None
 
-        zs = []
-        for m in range(B_TILES):
-            if m == B_TILES - 1:
-                next_shift = between(0, 1)
-            zs.append(result_of(0, m))
-            times_gain(banks[m][:], zs[m], ALL)
-            if m == B_TILES - 1:
-                quantise_if_any()
-            if m >= 1:
-                finish(0, m - 1, zs[m - 1], shift_ps)
-        quantise_if_any()
-        finish(0, B_TILES - 1, zs[B_TILES - 1], shift_ps)
+        behind = []
 
+        def empty_one_behind(bank, l, m, shift_ps):
+            z = result_of(l, m)
+            times_gain(bank[:], z, ALL)
+            catch_up()
+            behind.append((l, m, z, shift_ps))
+
+        def catch_up():
+            if behind:
+                finish(*behind.pop())
+
+        next_shift = between(0, 1)
+        for m in range(B_TILES):
+            empty_one_behind(banks[m], 0, m, shift_ps)
+            if m >= 1:
+                quantise_if_any()
+
+        X_DONE = LAST
         ALONE = 2
         for l in range(1, L - ALONE):
             shift_ps = next_shift
@@ -342,7 +340,12 @@ def tile_residualblock5_pa_t_e_kernel(tc, x, k1_words, k1_scales, b1, gamma1, be
                 banks = [psum_acc.tile([P, F], F32, name="acc") for k in range(2)]
                 taps_over_banks(banks, l, 2 * pair, LATER_TAPS, LATER_TAPS)
                 next_shift = between(l, pair)
-                empty_pair(banks, l, 2 * pair, shift_ps)
+                if l < X_DONE:
+                    for k in range(2):
+                        empty_one_behind(banks[k], l, 2 * pair + k, shift_ps)
+                        quantise_if_any()
+                else:
+                    empty_pair(banks, l, 2 * pair, shift_ps)
 
         def fill(l, m, cols):
             bank = psum_acc.tile([P, cols.stop - cols.start], F32, name="acc")
@@ -350,29 +353,43 @@ def tile_residualblock5_pa_t_e_kernel(tc, x, k1_words, k1_scales, b1, gamma1, be
                 product(bank, l, m, i, LATER_TAPS, cols)
             return bank
 
+        def gain_and_shift_in_halves(bank, z, shift_ps):
+            for cols in HALVES:
+                times_gain(bank[:, cols], z[:, cols], cols)
+            for cols in HALVES:
+                add_shift(z[:, cols], shift_ps, cols)
+
         l = L - 2
         shift_ps = next_shift
         for m in range(B_TILES):
             bank = fill(l, m, ALL)
             if m == B_TILES - 1:
                 next_shift = spread_row(L - 1)
-            empty_alone(bank, result_of(l, m), shift_ps)
+            z = result_of(l, m)
+            gain_and_shift_in_halves(bank, z, shift_ps)
+            bend_on_scalar_and_gpsimd(z)
             store_double(l, m)
 
         l = L - 1
         shift_ps = next_shift
+        singles = []
         for m in range(B_TILES - 1):
             bank = fill(l, m, ALL)
             single = results.tile([P, F], F32, tag="z")
-            empty_alone(bank, single[:], shift_ps)
-            nc.sync.dma_start(out=out_view[:, m, l, :], in_=single[:])
-        m = B_TILES - 1
+            singles.append(single)
+            gain_and_shift_in_halves(bank, single[:], shift_ps)
+            if m < B_TILES - 2:
+                bend_on_scalar_and_gpsimd(single[:])
+                nc.sync.dma_start(out=out_view[:, m, l, :], in_=single[:])
         single = results.tile([P, F], F32, tag="z")
+        singles.append(single)
         for cols in HALVES:
-            bank = fill(l, m, cols)
+            bank = fill(l, B_TILES - 1, cols)
             times_gain(bank[:], single[:, cols], cols)
         for cols in HALVES:
             add_shift(single[:, cols], shift_ps, cols)
+        bend_on_vector(singles[B_TILES - 2][:])
+        nc.sync.dma_start(out=out_view[:, B_TILES - 2, l, :], in_=singles[B_TILES - 2][:])
         for cols in HALVES:
             bend_on_vector(single[:, cols])
-            nc.sync.dma_start(out=out_view[:, m, l, cols], in_=single[:, cols])
+            nc.sync.dma_start(out=out_view[:, B_TILES - 1, l, cols], in_=single[:, cols])

@@ -103,10 +103,12 @@ def tile_residualblock5_pa_t_e_kernel(tc, x, k1_words, k1_scales, b1, gamma1, be
         load_x(0, 1)
         load_scales(0)
         load_w(0, 0, 1)
-        load_x(PAIRS - 1, 0)
         load_w(0, 1, 2)
+        load_w(0, 3, 4)
+        load_x(PAIRS - 1, 0)
         load_x(PAIRS - 1, 1)
-        load_w(0, 2, TAPS)
+        load_w(0, 2, 3)
+        load_w(0, 4, TAPS)
         load_x(1, 0)
         load_scales(1)
         load_w(1, 0, 2)
@@ -275,22 +277,19 @@ def tile_residualblock5_pa_t_e_kernel(tc, x, k1_words, k1_scales, b1, gamma1, be
         chunk(3, 0, nc.vector.tensor_copy)
         quantise_next()
         quantise_next()
-        sort_words(0, LAST)
-        sort_words(1, LAST)
         vectors_to_columns()
         nc.scalar.sqrt(out=std[:], in_=var_eps[:])
         for l in range(ZEROED_FIRST, L):
             zero_planes(l)
-        taps_over_banks(banks, 0, 0, (0,), FIRST_TAPS)
-        sort_words(2, LAST)
-        sort_words(3, LAST)
+        taps_over_banks(banks, 0, 0, (0, 1, 3), FIRST_TAPS)
+        gain_and_shift()
+        for m in range(B_TILES):
+            sort_words(m, LAST)
         chunk(0, LAST, nc.scalar.copy)
         chunk(1, LAST, nc.vector.tensor_copy)
         quantise_next()
-        gain_and_shift()
-        quantise_next()
-        taps_over_banks(banks, 0, 0, (1,), FIRST_TAPS)
         chunk(2, LAST, nc.scalar.copy)
+        quantise_next()
         chunk(3, LAST, nc.vector.tensor_copy)
         quantise_next()
         nc.scalar.copy(out=gain_bc[:], in_=spread_row(GAIN))
@@ -298,7 +297,7 @@ def tile_residualblock5_pa_t_e_kernel(tc, x, k1_words, k1_scales, b1, gamma1, be
         quantise_next()
         sort_words(0, 1)
         sort_words(1, 1)
-        taps_over_banks(banks, 0, 0, (3, 2, 4), FIRST_TAPS)
+        taps_over_banks(banks, 0, 0, (2, 4), FIRST_TAPS)
 
         def between(l, pair):
             newer = l + 1 if pair == 1 else l

@@ -47,7 +47,11 @@ def tile_residualblock5_pa_t_e_kernel(tc, x, k1_words, k1_scales, b1, gamma1, be
         x_codes = keep.tile([P, B_TILES, L, P], U32, align_bytes=64)
         x_scales = keep.tile([P, B_TILES, L, P], U8, align_bytes=64)
         w_codes = keep.tile([P, L, TAPS, F], U32, align_bytes=64)
-        w_scales = [keep.tile([P, TAPS, F], U8, align_bytes=64, name="w_scales_%d" % l) for l in range(L)]
+        PACKED = 4
+        w_scales = [keep.tile([P, F], U8, align_bytes=64, name="w_scales_%d" % l) for l in range(L)]
+        last_tap_scales = [
+            keep.tile([P, F], U8, align_bytes=64, name="last_tap_scales_%d" % h) for h in range(L // PACKED)
+        ]
         ident = keep.tile([P, P], F32)
         raw_bf = keep.tile([ROW_VAR + 1, F], BF16)
         raw = keep.tile([P, F], F32)
@@ -60,12 +64,8 @@ def tile_residualblock5_pa_t_e_kernel(tc, x, k1_words, k1_scales, b1, gamma1, be
 
         nc.vector.memset(raw[:], 0.0)
         nc.vector.memset(var_eps[:], 1.0)
-        def zero_planes(l):
-            nc.vector.memset(w_scales[l][:].rearrange("p i n -> p (i n)").bitcast(I32), 0)
-
-        ZEROED_FIRST = 6
-        for l in range(ZEROED_FIRST):
-            zero_planes(l)
+        for planes in w_scales[0:1] + last_tap_scales[0:1] + w_scales[1:L] + last_tap_scales[1:]:
+            nc.vector.memset(planes[:].bitcast(I32), 0)
         make_identity(nc, ident[:])
 
         nc.sync.dma_start(out=raw_bf[0:L, :], in_=b1)
@@ -75,7 +75,7 @@ def tile_residualblock5_pa_t_e_kernel(tc, x, k1_words, k1_scales, b1, gamma1, be
 
         x_view = x.rearrange("(m p) l c -> p m l c", p=P)
         w_view = k1_words.rearrange("(i l) p n t -> l p i (n t)", l=L)
-        s_view = k1_scales.rearrange("g (quad r) n -> r quad g n", r=4)
+        s_view = k1_scales.rearrange("(i l) q n -> l i q n", l=L)
         out_view = out.rearrange("(m p) l f -> p m l f", p=P)
 
         def load_x(pair, half):
@@ -85,9 +85,17 @@ def tile_residualblock5_pa_t_e_kernel(tc, x, k1_words, k1_scales, b1, gamma1, be
             )
 
         def load_scales(l):
-            for r in range(4):
+            for quad in range(4):
                 nc.sync.dma_start(
-                    out=w_scales[l][r:P:32, :, :].bitcast(I32), in_=s_view[r][:, l : TAPS * L : L, :].bitcast(I32)
+                    out=w_scales[l][32 * quad : 32 * quad + 4 * PACKED, :].bitcast(I32),
+                    in_=s_view[l][0:PACKED, 4 * quad : 4 * quad + 4, :].bitcast(I32),
+                )
+
+        def load_last_tap_scales(h):
+            for quad in range(4):
+                nc.sync.dma_start(
+                    out=last_tap_scales[h][32 * quad : 32 * quad + 4 * PACKED, :].bitcast(I32),
+                    in_=s_view[PACKED * h : PACKED * (h + 1), TAPS - 1, 4 * quad : 4 * quad + 4, :].bitcast(I32),
                 )
 
         def load_w(l, first, stop):
@@ -108,6 +116,7 @@ def tile_residualblock5_pa_t_e_kernel(tc, x, k1_words, k1_scales, b1, gamma1, be
         load_x(PAIRS - 1, 0)
         load_x(PAIRS - 1, 1)
         load_w(0, 2, 3)
+        load_last_tap_scales(0)
         load_w(0, 4, TAPS)
         load_x(1, 0)
         load_scales(1)
@@ -200,6 +209,11 @@ def tile_residualblock5_pa_t_e_kernel(tc, x, k1_words, k1_scales, b1, gamma1, be
 
         ALL = slice(0, F)
 
+        def scale_plane(l, i):
+            if i < PACKED:
+                return w_scales[l][4 * i : P, :]
+            return last_tap_scales[l // PACKED][4 * (l % PACKED) : P, :]
+
         def product(bank, l, m, i, taps, cols=ALL):
             src = (l - TAP_STEP[i]) % L
             nc.tensor.matmul_mx(
@@ -207,7 +221,7 @@ def tile_residualblock5_pa_t_e_kernel(tc, x, k1_words, k1_scales, b1, gamma1, be
                 lhsT=x_codes[:, m, src, :].bitcast(FP8X4),
                 lhsT_scale=x_scales[:, m, src, :],
                 rhs=w_codes[:, l, i, cols].bitcast(FP8X4),
-                rhs_scale=w_scales[l][:, i, cols],
+                rhs_scale=scale_plane(l, i)[:, cols],
                 start=(i == taps[0]),
                 stop=(i == taps[-1]),
             )
@@ -241,6 +255,8 @@ def tile_residualblock5_pa_t_e_kernel(tc, x, k1_words, k1_scales, b1, gamma1, be
                 nc.sync.dma_start(out=out_view[:, m - 1 : m + 1, l, :], in_=doubles[(l, m // 2)][:])
             if m == B_TILES - 1 and l + AHEAD < L:
                 load_scales(l + AHEAD)
+                if (l + AHEAD) % PACKED == 0:
+                    load_last_tap_scales((l + AHEAD) // PACKED)
                 load_w(l + AHEAD, 0, TAPS)
 
         def quantise_if_any():
@@ -279,8 +295,6 @@ def tile_residualblock5_pa_t_e_kernel(tc, x, k1_words, k1_scales, b1, gamma1, be
         quantise_next()
         vectors_to_columns()
         nc.scalar.sqrt(out=std[:], in_=var_eps[:])
-        for l in range(ZEROED_FIRST, L):
-            zero_planes(l)
         taps_over_banks(banks, 0, 0, (0, 1, 3), FIRST_TAPS)
         gain_and_shift()
         for m in range(B_TILES):

@@ -61,12 +61,24 @@ def tile_residualblock5_pa_t_e_kernel(tc, x, k1_words, k1_scales, b1, gamma1, be
         rstd = keep.tile([P, F_TILES], F32)
         spread = keep.tile([P, F_TILES, L + 1], F32)
         gain_bc = keep.tile([P, F], F32)
+        PIECES = 3
+        SPREAD = L + 1
+        pieces = keep.tile([P, F_TILES, P], BF16)
+        rest = keep.tile([P, F_TILES, SPREAD], F32)
+        piece_rows = keep.tile([P, F], BF16)
+        ident_bf = keep.tile([P, P], BF16)
+        pick_two = keep.tile([P, SPREAD], F32)
+        pick = keep.tile([P, SPREAD], BF16)
 
         nc.vector.memset(raw[:], 0.0)
         nc.vector.memset(var_eps[:], 1.0)
         for planes in w_scales[0:1] + last_tap_scales[0:1] + w_scales[1:L] + last_tap_scales[1:]:
             nc.vector.memset(planes[:].bitcast(I32), 0)
         make_identity(nc, ident[:])
+        make_identity(nc, ident_bf[:])
+        nc.gpsimd.memset(pieces[:], 0.0)
+        nc.gpsimd.tensor_tensor(out=pick_two[:], in0=ident[:, 0:SPREAD], in1=ident[:, SPREAD : 2 * SPREAD], op=ALU.add)
+        nc.gpsimd.tensor_tensor(out=pick[:], in0=pick_two[:], in1=ident[:, 2 * SPREAD : 3 * SPREAD], op=ALU.add)
 
         nc.sync.dma_start(out=raw_bf[0:L, :], in_=b1)
         for row, vec in ((ROW_GAMMA, gamma1), (ROW_BETA, beta1), (ROW_MEAN, mean1), (ROW_VAR, var1)):
@@ -191,11 +203,26 @@ def tile_residualblock5_pa_t_e_kernel(tc, x, k1_words, k1_scales, b1, gamma1, be
                 in1=cols[:, :, ROW_BETA : ROW_BETA + 1].to_broadcast(per_position),
             )
 
-        def spread_row(r):
-            row_ps = psum_row.tile([P, F_TILES, P], F32, tag="row")
+        def split_in_pieces():
+            for n in range(PIECES):
+                piece = pieces[:, :, n * SPREAD : (n + 1) * SPREAD]
+                whole = spread if n == 0 else rest
+                nc.vector.tensor_copy(out=piece, in_=whole[:])
+                if n < PIECES - 1:
+                    nc.vector.tensor_tensor(out=rest[:], in0=whole[:], in1=piece, op=ALU.subtract)
+
+        def pieces_to_rows():
+            rows_ps = psum_row.tile([P, F_TILES, P], BF16, tag="row")
             for j in range(F_TILES):
-                nc.tensor.transpose(row_ps[:, j, :], spread[:, j, r : r + 1].to_broadcast([P, P]), ident[:])
-            return row_ps[:].rearrange("p j n -> p (j n)")
+                nc.tensor.transpose(rows_ps[:, j, :], pieces[:, j, :], ident_bf[:])
+            nc.scalar.copy(out=piece_rows[:], in_=rows_ps[:].rearrange("p j n -> p (j n)"))
+
+        def spread_row(r):
+            row_ps = psum_row.tile([P, F], F32, tag="row")
+            nc.tensor.matmul(
+                out=row_ps[:], lhsT=pick[:, r : r + 1].to_broadcast([P, P]), rhs=piece_rows[:], start=True, stop=True
+            )
+            return row_ps[:]
 
         waiting = []
         quantised = [0]
@@ -285,7 +312,9 @@ def tile_residualblock5_pa_t_e_kernel(tc, x, k1_words, k1_scales, b1, gamma1, be
         LAST = PAIRS - 1
         banks = [psum_acc.tile([P, F], F32, name="acc") for m in range(B_TILES)]
         nc.vector.tensor_copy(out=raw[0 : ROW_VAR + 1, :], in_=raw_bf[:])
+        vectors_to_columns()
         chunk(0, 0, nc.scalar.copy)
+        nc.scalar.sqrt(out=std[:], in_=var_eps[:])
         chunk(1, 0, nc.vector.tensor_copy)
         quantise_next()
         chunk(2, 0, nc.scalar.copy)
@@ -293,15 +322,15 @@ def tile_residualblock5_pa_t_e_kernel(tc, x, k1_words, k1_scales, b1, gamma1, be
         chunk(3, 0, nc.vector.tensor_copy)
         quantise_next()
         quantise_next()
-        vectors_to_columns()
-        nc.scalar.sqrt(out=std[:], in_=var_eps[:])
         taps_over_banks(banks, 0, 0, (0, 1, 3), FIRST_TAPS)
         gain_and_shift()
+        split_in_pieces()
         for m in range(B_TILES):
             sort_words(m, LAST)
         chunk(0, LAST, nc.scalar.copy)
         chunk(1, LAST, nc.vector.tensor_copy)
         quantise_next()
+        pieces_to_rows()
         chunk(2, LAST, nc.scalar.copy)
         quantise_next()
         chunk(3, LAST, nc.vector.tensor_copy)

@@ -80,9 +80,11 @@ def tile_residualblock5_pa_t_e_kernel(tc, x, k1_words, k1_scales, b1, gamma1, be
         nc.gpsimd.tensor_tensor(out=pick_two[:], in0=ident[:, 0:SPREAD], in1=ident[:, SPREAD : 2 * SPREAD], op=ALU.add)
         nc.gpsimd.tensor_tensor(out=pick[:], in0=pick_two[:], in1=ident[:, 2 * SPREAD : 3 * SPREAD], op=ALU.add)
 
-        nc.sync.dma_start(out=raw_bf[0:L, :], in_=b1)
-        for row, vec in ((ROW_GAMMA, gamma1), (ROW_BETA, beta1), (ROW_MEAN, mean1), (ROW_VAR, var1)):
-            nc.sync.dma_start(out=raw_bf[row : row + 1, :], in_=vec.unsqueeze(0))
+        def load_small_vectors():
+            nc.sync.dma_start(out=raw_bf[0:L, :], in_=b1)
+            for row, vec in ((ROW_GAMMA, gamma1), (ROW_BETA, beta1), (ROW_MEAN, mean1), (ROW_VAR, var1)):
+                nc.sync.dma_start(out=raw_bf[row : row + 1, :], in_=vec.unsqueeze(0))
+
         nc.scalar.sqrt(out=std[:], in_=var_eps[:])
 
         x_view = x.rearrange("(m p) l c -> p m l c", p=P)
@@ -120,6 +122,7 @@ def tile_residualblock5_pa_t_e_kernel(tc, x, k1_words, k1_scales, b1, gamma1, be
         AHEAD = 4
 
         load_x(0, 0)
+        load_small_vectors()
         load_x(0, 1)
         load_scales(0)
         load_w(0, 0, 1)
@@ -301,8 +304,15 @@ def tile_residualblock5_pa_t_e_kernel(tc, x, k1_words, k1_scales, b1, gamma1, be
                 pair_z.append(result_of(l, first_m + k))
                 times_gain(banks[k][:], pair_z[k], ALL)
                 catch_up()
-            for k in range(2):
-                finish(l, first_m + k, pair_z[k], shift_ps)
+            if first_m + 1 == B_TILES - 1:
+                add_shift(pair_z[1], shift_ps, ALL)
+                add_shift(pair_z[0], shift_ps, ALL)
+                bend_on_scalar_and_gpsimd(pair_z[0])
+                bend_on_vector(pair_z[1])
+                store_double(l, first_m + 1)
+            else:
+                for k in range(2):
+                    finish(l, first_m + k, pair_z[k], shift_ps)
 
         def taps_over_banks(banks, l, first_m, taps, all_taps):
             for i in taps:
@@ -311,13 +321,13 @@ def tile_residualblock5_pa_t_e_kernel(tc, x, k1_words, k1_scales, b1, gamma1, be
 
         LAST = PAIRS - 1
         banks = [psum_acc.tile([P, F], F32, name="acc") for m in range(B_TILES)]
-        nc.vector.tensor_copy(out=raw[0 : ROW_VAR + 1, :], in_=raw_bf[:])
-        vectors_to_columns()
         chunk(0, 0, nc.scalar.copy)
-        nc.scalar.sqrt(out=std[:], in_=var_eps[:])
+        nc.vector.tensor_copy(out=raw[0 : ROW_VAR + 1, :], in_=raw_bf[:])
         chunk(1, 0, nc.vector.tensor_copy)
         quantise_next()
+        vectors_to_columns()
         chunk(2, 0, nc.scalar.copy)
+        nc.scalar.sqrt(out=std[:], in_=var_eps[:])
         quantise_next()
         chunk(3, 0, nc.vector.tensor_copy)
         quantise_next()
@@ -380,8 +390,9 @@ def tile_residualblock5_pa_t_e_kernel(tc, x, k1_words, k1_scales, b1, gamma1, be
             shift_ps = next_shift
             for pair in range(B_TILES // 2):
                 banks = [psum_acc.tile([P, F], F32, name="acc") for k in range(2)]
-                taps_over_banks(banks, l, 2 * pair, LATER_TAPS, LATER_TAPS)
+                taps_over_banks(banks, l, 2 * pair, LATER_TAPS[0 : TAPS - 1], LATER_TAPS)
                 next_shift = between(l, pair)
+                taps_over_banks(banks, l, 2 * pair, LATER_TAPS[TAPS - 1 : TAPS], LATER_TAPS)
                 if l < X_DONE:
                     for k in range(2):
                         empty_one_behind(banks[k], l, 2 * pair + k, shift_ps)
@@ -409,7 +420,11 @@ def tile_residualblock5_pa_t_e_kernel(tc, x, k1_words, k1_scales, b1, gamma1, be
                 next_shift = spread_row(L - 1)
             z = result_of(l, m)
             gain_and_shift_in_halves(bank, z, shift_ps)
-            bend_on_scalar_and_gpsimd(z)
+            if m == B_TILES - 1:
+                for cols in HALVES:
+                    bend_on_vector(z[:, cols])
+            else:
+                bend_on_scalar_and_gpsimd(z)
             store_double(l, m)
 
         l = L - 1

from contextlib import ExitStack

import concourse.mybir as mybir
from concourse.masks import make_identity

F32 = mybir.dt.float32
BF16 = mybir.dt.bfloat16
I32 = mybir.dt.int32
U32 = mybir.dt.uint32
U8 = mybir.dt.uint8
FP8X4 = mybir.dt.float8_e4m3fn_x4
ALU = mybir.AluOpType
ACT = mybir.ActivationFunctionType

P = 128
PACK = 4
B, L, C, F = 512, 8, 512, 512
TAP_STEP = (0, 0, 1, -1, 2)
TAPS = len(TAP_STEP)
B_TILES = B // P
F_TILES = F // P
PAIRS = L // 2
BN_EPS = 1e-3
LEAKY_ALPHA = 0.3

FLOPS = 2 * TAPS * L * B * C * F

ROW_GAMMA, ROW_BETA, ROW_MEAN, ROW_VAR, ROWS = 8, 9, 10, 11, 16
GAIN = L


def tile_residualblock5_pa_t_e_kernel(tc, x, k1_words, k1_scales, b1, gamma1, beta1, mean1, var1, out):
    nc = tc.nc

    with ExitStack() as ctx:
        ctx.enter_context(tc.manual_schedule())
        keep = ctx.enter_context(tc.tile_pool(name="keep", bufs=1))
        stage = ctx.enter_context(tc.tile_pool(name="stage", bufs=4))
        sorting = ctx.enter_context(tc.tile_pool(name="sorting", bufs=4))
        results = ctx.enter_context(tc.tile_pool(name="results", bufs=8))
        scratch = ctx.enter_context(tc.tile_pool(name="scratch", bufs=3))
        psum_xt = ctx.enter_context(tc.psum_pool(name="psum_xt", bufs=2))
        psum_row = ctx.enter_context(tc.psum_pool(name="psum_row", bufs=2))
        psum_acc = ctx.enter_context(tc.psum_pool(name="psum_acc", bufs=4))

        x_sb = keep.tile([P, PAIRS, B_TILES, 2, C], BF16)
        x_codes = keep.tile([P, B_TILES, L, P], U32, align_bytes=64)
        x_scales = keep.tile([P, B_TILES, L, P], U8, align_bytes=64)
        w_codes = keep.tile([P, L, TAPS, F], U32, align_bytes=64)
        PACKED = 4
        w_scales = [keep.tile([P, F], U8, align_bytes=64, name="w_scales_%d" % l) for l in range(L)]
        last_tap_scales = [
            keep.tile([P, F], U8, align_bytes=64, name="last_tap_scales_%d" % h) for h in range(L // PACKED)
        ]
        ident = keep.tile([P, P], F32)
        raw_bf = keep.tile([ROW_VAR + 1, F], BF16)
        raw = keep.tile([P, F], F32)
        cols = keep.tile([P, F_TILES, ROWS], F32)
        var_eps = keep.tile([P, F_TILES], F32)
        std = keep.tile([P, F_TILES], F32)
        rstd = keep.tile([P, F_TILES], F32)
        spread = keep.tile([P, F_TILES, L + 1], F32)
        gain_bc = keep.tile([P, F], F32)
        PIECES = 3
        SPREAD = L + 1
        pieces = keep.tile([P, F_TILES, P], BF16)
        rest = keep.tile([P, F_TILES, SPREAD], F32)
        piece_rows = keep.tile([P, F], BF16)
        ident_bf = keep.tile([P, P], BF16)
        pick_two = keep.tile([P, SPREAD], F32)
        pick = keep.tile([P, SPREAD], BF16)

        nc.vector.memset(raw[:], 0.0)
        nc.vector.memset(var_eps[:], 1.0)
        for planes in w_scales[0:1] + last_tap_scales[0:1] + w_scales[1:L] + last_tap_scales[1:]:
            nc.vector.memset(planes[:].bitcast(I32), 0)
        make_identity(nc, ident[:])
        make_identity(nc, ident_bf[:])
        nc.gpsimd.memset(pieces[:], 0.0)
        nc.gpsimd.tensor_tensor(out=pick_two[:], in0=ident[:, 0:SPREAD], in1=ident[:, SPREAD : 2 * SPREAD], op=ALU.add)
        nc.gpsimd.tensor_tensor(out=pick[:], in0=pick_two[:], in1=ident[:, 2 * SPREAD : 3 * SPREAD], op=ALU.add)

        def load_small_vectors():
            nc.sync.dma_start(out=raw_bf[0:L, :], in_=b1)
            for row, vec in ((ROW_GAMMA, gamma1), (ROW_BETA, beta1), (ROW_MEAN, mean1), (ROW_VAR, var1)):
                nc.sync.dma_start(out=raw_bf[row : row + 1, :], in_=vec.unsqueeze(0))

        nc.scalar.sqrt(out=std[:], in_=var_eps[:])

        x_view = x.rearrange("(m p) l c -> p m l c", p=P)
        w_view = k1_words.rearrange("(i l) p n t -> l p i (n t)", l=L)
        s_view = k1_scales.rearrange("(i l) q n -> l i q n", l=L)
        out_view = out.rearrange("(m p) l f -> p m l f", p=P)

        def load_x(pair, half):
            nc.sync.dma_start(
                out=x_sb[:, pair, 2 * half : 2 * half + 2, :, :],
                in_=x_view[:, 2 * half : 2 * half + 2, 2 * pair : 2 * pair + 2, :],
            )

        def load_scales(l):
            for quad in range(4):
                nc.sync.dma_start(
                    out=w_scales[l][32 * quad : 32 * quad + 4 * PACKED, :].bitcast(I32),
                    in_=s_view[l][0:PACKED, 4 * quad : 4 * quad + 4, :].bitcast(I32),
                )

        def load_last_tap_scales(h):
            for quad in range(4):
                nc.sync.dma_start(
                    out=last_tap_scales[h][32 * quad : 32 * quad + 4 * PACKED, :].bitcast(I32),
                    in_=s_view[PACKED * h : PACKED * (h + 1), TAPS - 1, 4 * quad : 4 * quad + 4, :].bitcast(I32),
                )

        def load_w(l, first, stop):
            nc.sync.dma_start(
                out=w_codes[:, l, first:stop, :].bitcast(I32), in_=w_view[l][:, first:stop, :].bitcast(I32)
            )

        FIRST_TAPS = (0, 1, 3, 2, 4)
        LATER_TAPS = (0, 1, 2, 4, 3)
        AHEAD = 4

        load_x(0, 0)
        load_small_vectors()
        load_x(0, 1)
        load_scales(0)
        load_w(0, 0, 1)
        load_w(0, 1, 2)
        load_w(0, 3, 4)
        load_x(PAIRS - 1, 0)
        load_x(PAIRS - 1, 1)
        load_w(0, 2, 3)
        load_last_tap_scales(0)
        load_w(0, 4, TAPS)
        load_x(1, 0)
        load_scales(1)
        load_w(1, 0, 2)
        load_w(1, 2, TAPS)
        load_x(1, 1)
        load_scales(2)
        load_w(2, 0, TAPS)
        load_x(2, 0)
        load_x(2, 1)
        load_scales(3)
        load_w(3, 0, TAPS)

        sorted_words = {}

        def sort_words(m, pair):
            by_parity = sorting.tile([P, 2, 2, P], F32)
            nc.scalar.copy(
                out=by_parity[:],
                in_=x_sb[:, pair, m, :, :].bitcast(F32).rearrange("p l (j u) -> p l u j", u=2),
            )
            sorted_words[(m, pair)] = by_parity

        def transpose_chunk(m, pair, copy):
            xt = psum_xt.tile([P, 2, 2, P], F32, tag="xt")
            for li in range(2):
                words = x_sb[:, pair, m, li, :].bitcast(F32)
                for u in range(2):
                    if (m, pair) in sorted_words:
                        nc.tensor.transpose(xt[:, li, u, :], sorted_words[(m, pair)][:, li, u, :], ident[:])
                    else:
                        nc.tensor.transpose(xt[:, li, u, :], words[:, u : C // 2 : 2], ident[:])
            grouped = stage.tile([P, 2, P, PACK], BF16, align_bytes=64)
            copy(out=grouped[:].bitcast(F32), in_=xt[:].rearrange("p l u b -> p l b u"))
            return (m, pair, grouped)

        def quantise_chunk(m, pair, grouped):
            ls = slice(2 * pair, 2 * pair + 2)
            nc.vector.quantize_mx(
                out=x_codes[:, m, ls, :].rearrange("p l b -> p (l b)").bitcast(FP8X4),
                scales=x_scales[:, m, ls, :].rearrange("p l b -> p (l b)"),
                in_=grouped[:].rearrange("p l b t -> p (l b t)"),
            )

        def vectors_to_columns():
            cols_ps = psum_row.tile([P, F_TILES, P], F32, tag="row")
            for j in range(F_TILES):
                nc.tensor.transpose(cols_ps[:, j, :], raw[:, j * P : (j + 1) * P], ident[:])
            nc.vector.tensor_copy(out=cols[:], in_=cols_ps[:, :, 0:ROWS])
            nc.vector.tensor_scalar_add(out=var_eps[:], in0=cols[:, :, ROW_VAR], scalar1=BN_EPS)

        def gain_and_shift():
            per_position = [P, F_TILES, L]
            nc.vector.reciprocal(out=rstd[:], in_=std[:])
            nc.vector.tensor_mul(out=spread[:, :, GAIN], in0=cols[:, :, ROW_GAMMA], in1=rstd[:])
            nc.vector.scalar_tensor_tensor(
                out=spread[:, :, 0:L],
                in0=cols[:, :, 0:L],
                scalar=2.0,
                in1=cols[:, :, ROW_MEAN : ROW_MEAN + 1].to_broadcast(per_position),
                op0=ALU.mult,
                op1=ALU.subtract,
            )
            nc.vector.tensor_mul(
                out=spread[:, :, 0:L],
                in0=spread[:, :, 0:L],
                in1=spread[:, :, GAIN : GAIN + 1].to_broadcast(per_position),
            )
            nc.vector.tensor_add(
                out=spread[:, :, 0:L],
                in0=spread[:, :, 0:L],
                in1=cols[:, :, ROW_BETA : ROW_BETA + 1].to_broadcast(per_position),
            )

        def split_in_pieces():
            for n in range(PIECES):
                piece = pieces[:, :, n * SPREAD : (n + 1) * SPREAD]
                whole = spread if n == 0 else rest
                nc.vector.tensor_copy(out=piece, in_=whole[:])
                if n < PIECES - 1:
                    nc.vector.tensor_tensor(out=rest[:], in0=whole[:], in1=piece, op=ALU.subtract)

        def pieces_to_rows():
            rows_ps = psum_row.tile([P, F_TILES, P], BF16, tag="row")
            for j in range(F_TILES):
                nc.tensor.transpose(rows_ps[:, j, :], pieces[:, j, :], ident_bf[:])
            nc.scalar.copy(out=piece_rows[:], in_=rows_ps[:].rearrange("p j n -> p (j n)"))

        def spread_row(r):
            row_ps = psum_row.tile([P, F], F32, tag="row")
            nc.tensor.matmul(
                out=row_ps[:], lhsT=pick[:, r : r + 1].to_broadcast([P, P]), rhs=piece_rows[:], start=True, stop=True
            )
            return row_ps[:]

        waiting = []
        quantised = [0]

        def quantise_next():
            quantise_chunk(*waiting[quantised[0]])
            quantised[0] += 1

        def chunk(m, pair, copy):
            waiting.append(transpose_chunk(m, pair, copy))

        ALL = slice(0, F)

        def scale_plane(l, i):
            if i < PACKED:
                return w_scales[l][4 * i : P, :]
            return last_tap_scales[l // PACKED][4 * (l % PACKED) : P, :]

        def product(bank, l, m, i, taps, cols=ALL):
            src = (l - TAP_STEP[i]) % L
            nc.tensor.matmul_mx(
                out=bank[:],
                lhsT=x_codes[:, m, src, :].bitcast(FP8X4),
                lhsT_scale=x_scales[:, m, src, :],
                rhs=w_codes[:, l, i, cols].bitcast(FP8X4),
                rhs_scale=scale_plane(l, i)[:, cols],
                start=(i == taps[0]),
                stop=(i == taps[-1]),
            )

        HALVES = (slice(0, F // 2), slice(F // 2, F))

        def times_gain(bank, z, cols):
            nc.vector.tensor_tensor(out=z, in0=bank, in1=gain_bc[:, cols], op=ALU.mult)

        def add_shift(z, shift_ps, cols):
            nc.vector.tensor_tensor(out=z, in0=z, in1=shift_ps[:, cols], op=ALU.add)

        def bend_on_scalar_and_gpsimd(z):
            lift = scratch.tile([P, F], F32, tag="lift")
            nc.scalar.activation(out=lift[:], in_=z, func=ACT.Relu, scale=LEAKY_ALPHA - 1.0)
            nc.gpsimd.tensor_tensor(out=z, in0=z, in1=lift[:], op=ALU.add)

        def bend_on_vector(z):
            nc.vector.scalar_tensor_tensor(out=z, in0=z, scalar=LEAKY_ALPHA, in1=z, op0=ALU.mult, op1=ALU.max)

        doubles = {}

        def result_of(l, m):
            if m % 2 == 0:
                double = results.tile([P, 2, F], F32, tag="z")
                doubles[(l, m // 2)] = double
            return doubles[(l, m // 2)][:, m % 2, :]

        def store_double(l, m):
            if m % 2 == 1:
                nc.sync.dma_start(out=out_view[:, m - 1 : m + 1, l, :], in_=doubles[(l, m // 2)][:])
            if m == B_TILES - 1 and l + AHEAD < L:
                load_scales(l + AHEAD)
                if (l + AHEAD) % PACKED == 0:
                    load_last_tap_scales((l + AHEAD) // PACKED)
                load_w(l + AHEAD, 0, TAPS)

        def quantise_if_any():
            if quantised[0] < len(waiting):
                quantise_next()

        def finish(l, m, z, shift_ps):
            add_shift(z, shift_ps, ALL)
            bend_on_scalar_and_gpsimd(z)
            store_double(l, m)

        def empty_pair(banks, l, first_m, shift_ps):
            pair_z = []
            for k in range(2):
                pair_z.append(result_of(l, first_m + k))
                times_gain(banks[k][:], pair_z[k], ALL)
                catch_up()
            if first_m + 1 == B_TILES - 1:
                add_shift(pair_z[1], shift_ps, ALL)
                add_shift(pair_z[0], shift_ps, ALL)
                bend_on_scalar_and_gpsimd(pair_z[0])
                bend_on_vector(pair_z[1])
                store_double(l, first_m + 1)
            else:
                for k in range(2):
                    finish(l, first_m + k, pair_z[k], shift_ps)

        def taps_over_banks(banks, l, first_m, taps, all_taps):
            for i in taps:
                for k in range(len(banks)):
                    product(banks[k], l, first_m + k, i, all_taps)

        LAST = PAIRS - 1
        banks = [psum_acc.tile([P, F], F32, name="acc") for m in range(B_TILES)]
        chunk(0, 0, nc.scalar.copy)
        nc.vector.tensor_copy(out=raw[0 : ROW_VAR + 1, :], in_=raw_bf[:])
        chunk(1, 0, nc.vector.tensor_copy)
        quantise_next()
        vectors_to_columns()
        chunk(2, 0, nc.scalar.copy)
        nc.scalar.sqrt(out=std[:], in_=var_eps[:])
        quantise_next()
        chunk(3, 0, nc.vector.tensor_copy)
        quantise_next()
        quantise_next()
        taps_over_banks(banks, 0, 0, (0, 1, 3), FIRST_TAPS)
        gain_and_shift()
        split_in_pieces()
        for m in range(B_TILES):
            sort_words(m, LAST)
        chunk(0, LAST, nc.scalar.copy)
        chunk(1, LAST, nc.vector.tensor_copy)
        quantise_next()
        pieces_to_rows()
        chunk(2, LAST, nc.scalar.copy)
        quantise_next()
        chunk(3, LAST, nc.vector.tensor_copy)
        quantise_next()
        nc.scalar.copy(out=gain_bc[:], in_=spread_row(GAIN))
        shift_ps = spread_row(0)
        quantise_next()
        sort_words(0, 1)
        sort_words(1, 1)
        taps_over_banks(banks, 0, 0, (2, 4), FIRST_TAPS)

        def between(l, pair):
            newer = l + 1 if pair == 1 else l
            if 1 <= newer < LAST:
                first_m = 0 if pair == 1 else 2
                chunk(first_m, newer, nc.scalar.copy)
                chunk(first_m + 1, newer, nc.scalar.copy)
                after = (2, newer) if pair == 1 else (0, newer + 1)
                if after[1] < LAST:
                    sort_words(after[0], after[1])
                    sort_words(after[0] + 1, after[1])
            if pair == 1 and l + 1 < L:
                return spread_row(l + 1)
            return None

        behind = []

        def empty_one_behind(bank, l, m, shift_ps):
            z = result_of(l, m)
            times_gain(bank[:], z, ALL)
            catch_up()
            behind.append((l, m, z, shift_ps))

        def catch_up():
            if behind:
                finish(*behind.pop())

        next_shift = between(0, 1)
        for m in range(B_TILES):
            empty_one_behind(banks[m], 0, m, shift_ps)
            if m >= 1:
                quantise_if_any()

        X_DONE = LAST
        ALONE = 2
        for l in range(1, L - ALONE):
            shift_ps = next_shift
            for pair in range(B_TILES // 2):
                banks = [psum_acc.tile([P, F], F32, name="acc") for k in range(2)]
                taps_over_banks(banks, l, 2 * pair, LATER_TAPS[0 : TAPS - 1], LATER_TAPS)
                next_shift = between(l, pair)
                taps_over_banks(banks, l, 2 * pair, LATER_TAPS[TAPS - 1 : TAPS], LATER_TAPS)
                if l < X_DONE:
                    for k in range(2):
                        empty_one_behind(banks[k], l, 2 * pair + k, shift_ps)
                        quantise_if_any()
                else:
                    empty_pair(banks, l, 2 * pair, shift_ps)

        def fill(l, m, cols):
            bank = psum_acc.tile([P, cols.stop - cols.start], F32, name="acc")
            for i in LATER_TAPS:
                product(bank, l, m, i, LATER_TAPS, cols)
            return bank

        def gain_and_shift_in_halves(bank, z, shift_ps):
            for cols in HALVES:
                times_gain(bank[:, cols], z[:, cols], cols)
            for cols in HALVES:
                add_shift(z[:, cols], shift_ps, cols)

        l = L - 2
        shift_ps = next_shift
        for m in range(B_TILES):
            bank = fill(l, m, ALL)
            if m == B_TILES - 1:
                next_shift = spread_row(L - 1)
            z = result_of(l, m)
            gain_and_shift_in_halves(bank, z, shift_ps)
            if m == B_TILES - 1:
                for cols in HALVES:
                    bend_on_vector(z[:, cols])
            else:
                bend_on_scalar_and_gpsimd(z)
            store_double(l, m)

        l = L - 1
        shift_ps = next_shift
        singles = []
        for m in range(B_TILES - 1):
            bank = fill(l, m, ALL)
            single = results.tile([P, F], F32, tag="z")
            singles.append(single)
            gain_and_shift_in_halves(bank, single[:], shift_ps)
            if m < B_TILES - 2:
                bend_on_scalar_and_gpsimd(single[:])
                nc.sync.dma_start(out=out_view[:, m, l, :], in_=single[:])
        single = results.tile([P, F], F32, tag="z")
        singles.append(single)
        for cols in HALVES:
            bank = fill(l, B_TILES - 1, cols)
            times_gain(bank[:], single[:, cols], cols)
        for cols in HALVES:
            add_shift(single[:, cols], shift_ps, cols)
        bend_on_vector(singles[B_TILES - 2][:])
        nc.sync.dma_start(out=out_view[:, B_TILES - 2, l, :], in_=singles[B_TILES - 2][:])
        for cols in HALVES:
            bend_on_vector(single[:, cols])
            nc.sync.dma_start(out=out_view[:, B_TILES - 1, l, cols], in_=single[:, cols])
